import numpy as np
import ml_dtypes


def mxq(x, axis, fmt="e4m3"):
    dtype, down = {"e4m3": (ml_dtypes.float8_e4m3fn, 7), "e5m2": (ml_dtypes.float8_e5m2, 14)}[fmt]
    v = np.moveaxis(np.asarray(x, np.float32).astype(ml_dtypes.bfloat16).astype(np.float64), axis, -1)
    blocks = v.reshape(v.shape[:-1] + (-1, 32))
    amax = np.abs(blocks).max(-1, keepdims=True)
    byte = np.maximum(np.where(amax > 0, np.frexp(amax)[1] - 1 + 127, 0) - down, 1)
    scale = np.exp2(byte - 127.0)
    codes = (blocks / scale).astype(np.float32).astype(dtype).astype(np.float64)
    return np.moveaxis((codes * scale).reshape(v.shape), -1, axis)


WIDE = False


def mx_kscale(k):
    if not WIDE:
        return np.ones(k)
    levels = np.array([10, -10, 5, -5, 0])
    a = np.random.permutation(np.resize(levels, k // 512 * 4)).reshape(k // 512, 4)
    idx = np.arange(k)
    return np.exp2(a[idx // 512, idx % 128 // 32])


BF16 = ml_dtypes.bfloat16


def bf(x):
    return np.asarray(x, np.float32).astype(BF16)


def f64(x):
    return np.asarray(x).astype(np.float64)


E2M1 = np.array([0.0, 0.5, 1.0, 1.5, 2.0, 3.0, 4.0, 6.0, -0.0, -0.5, -1.0, -1.5, -2.0, -3.0, -4.0, -6.0])


def pack_weight(w, fmt):
    k, n = w.shape
    w = f64(bf(w)).reshape(k // 32, 32, n)
    amax = np.abs(w).max(1)
    if fmt == "e4m3":
        byte = np.frexp(amax)[1] - 1 + 127 - 7
    else:
        mant, ex = np.frexp(amax / 6.0)
        byte = np.where(mant > 0.5, ex, ex - 1) + 127
    byte = np.clip(np.where(amax > 0, byte, 1), 1, 254)
    scaled = (w * np.exp2(127.0 - byte)[:, None, :]).reshape(k, n).astype(np.float32)
    by_word = np.ascontiguousarray(scaled.reshape(k // 512, 128, 4, n).transpose(0, 1, 3, 2))
    if fmt == "e4m3":
        words = by_word.astype(ml_dtypes.float8_e4m3fn).view(np.uint8)
    else:
        c = by_word.astype(ml_dtypes.float4_e2m1fn).view(np.uint8) & 0xF
        words = c[..., 0::2] | (c[..., 1::2] << 4)
    return np.ascontiguousarray(words), np.ascontiguousarray(byte.astype(np.uint8).reshape(k // 512, 16, n))


def unpack_weight(words, scales, fmt):
    g, p, n, _ = words.shape
    if fmt == "e4m3":
        vals = np.ascontiguousarray(words).view(ml_dtypes.float8_e4m3fn).astype(np.float64)
    else:
        nib = np.empty((g, p, n, 4), np.uint8)
        nib[..., 0::2] = words & 0xF
        nib[..., 1::2] = words >> 4
        vals = E2M1[nib]
    vals = vals * np.repeat(np.exp2(scales.astype(np.float64) - 127.0), 8, axis=1)[..., None]
    return vals.transpose(0, 1, 3, 2).reshape(g * 512, n)

def pack4(w):
    words, scales = pack_weight(w, "e2m1")
    return words.reshape(words.shape[0], 128, -1), scales


def unpack4(words, scales):
    return unpack_weight(words.reshape(words.shape[0], 128, -1, 2), scales, "e2m1")


B, C, H, W = 128, 1024, 3, 3
C3, P = 3 * C, H * W
EPS = 1e-5


def setup_inputs():
    s = mx_kscale(C3)
    n = np.random.standard_normal
    fv = bf(n((B, C3, H, W)) * s[None, :, None, None])
    ft = bf(n((B, C)))
    W1_words, W1_scales = pack4((n((C, C3)) / np.sqrt(C3) / s[None, :]).T)
    return {
        "fv": fv,
        "ft": ft,
        "W1_words": W1_words,
        "W1_scales": W1_scales,
        "b1": bf(n(C) * 0.3),
        "g1": bf(1.0 + 0.1 * n(C)),
        "be1": bf(n(C) * 0.3),
        "m1": bf(n(C) * 0.3),
        "v1": bf(np.random.uniform(0.5, 1.5, C)),
        "Wfc1": bf(n((C, C)) * 0.7 / np.sqrt(C)),
        "bfc1": bf(n(C) * 0.3),
    }


def reference(fv, ft, W1_words, W1_scales, b1, g1, be1, m1, v1, Wfc1, bfc1):
    x = (unpack4(W1_words, W1_scales).T @ mxq(f64(fv).reshape(B, C3, P), 1, "e4m3")) + f64(b1)[None, :, None]
    s = f64(g1) / np.sqrt(f64(v1) + EPS)
    fv1 = np.maximum(x * s[None, :, None] + (f64(be1) - f64(m1) * s)[None, :, None], 0.0)
    ft1 = f64(ft) @ f64(Wfc1).T + f64(bfc1)
    out = fv1 + fv1 * ft1[:, :, None]
    return out.reshape(B, C, H, W)

@@ -1,0 +1,226 @@
+from contextlib import ExitStack
+
+import concourse.mybir as mybir
+from concourse.masks import make_identity
+
+F32 = mybir.dt.float32
+BF16 = mybir.dt.bfloat16
+I32 = mybir.dt.int32
+U32 = mybir.dt.uint32
+U8 = mybir.dt.uint8
+FP8X4 = mybir.dt.float8_e4m3fn_x4
+FP4X4 = mybir.dt.float4_e2m1fn_x4
+ALU = mybir.AluOpType
+ACT = mybir.ActivationFunctionType
+
+P = 128
+C_IN = 3072
+C_OUT = 1024
+C_TXT = 1024
+PIX = 9
+EPS = 1e-5
+PACK = 4
+K_PASS = P * PACK
+PASSES = C_IN // K_PASS
+N_TILE = 512
+HALVES = C_OUT // N_TILE
+PAIRS = (PIX + 1) // 2
+ODD_PITCH = 2 * PAIRS
+O_STORE = 128
+
+FLOPS = 2 * P * PIX * C_IN * C_OUT + 2 * P * C_TXT * C_OUT
+
+
+def tile_joint_module_pa_kernel(
+    tc, fv, ft, W1_words, W1_scales, b1, g1, be1, m1, v1, Wfc1, bfc1, out
+):
+    nc = tc.nc
+    fv_rows = fv.rearrange("b c h w -> b (c h w)")
+    out_rows = out.rearrange("b o h w -> b (o h w)")
+    chunk = K_PASS * PIX
+
+    with ExitStack() as ctx:
+        keep = ctx.enter_context(tc.tile_pool(name="keep", bufs=1))
+        psum = ctx.enter_context(tc.psum_pool(name="psum", bufs=8))
+
+        vectors = [b1, g1, be1, m1, v1, bfc1]
+        rows = C_OUT // P
+        k_tiles = C_TXT // P
+
+        w_words = keep.tile([P, PASSES, 2 * C_OUT], U8, align_bytes=64)
+        fv_codes = keep.tile([P, PASSES, PIX * P], U32, align_bytes=64)
+        fv_scales = keep.tile([P, PASSES, PIX * P], U8, align_bytes=64)
+        cols = keep.tile([P, len(vectors), rows], F32)
+        std = keep.tile([P, rows], F32)
+        rstd = keep.tile([P, rows], F32)
+        trio = keep.tile([P, 3, rows], F32)
+        spread = keep.tile([P, 3, C_OUT], F32)
+        ftT = keep.tile([P, k_tiles, P], BF16)
+        wfcT = keep.tile([P, k_tiles, C_OUT], BF16)
+        gate = keep.tile([P, C_OUT], F32)
+
+        ident_bf = keep.tile([P, P], BF16)
+        make_identity(nc, ident_bf[:])
+        ident_f32 = keep.tile([P, P], F32)
+        make_identity(nc, ident_f32[:])
+
+        vec_rows = keep.tile([P, P], BF16)
+        nc.vector.memset(vec_rows[:], 0.0)
+        w_scales = keep.tile([P, PASSES, C_OUT], U8, align_bytes=64)
+        nc.vector.memset(w_scales[:].rearrange("p g n -> p (g n)").bitcast(I32), 0)
+
+        for v, vector in enumerate(vectors):
+            nc.scalar.dma_start(
+                out=vec_rows[rows * v : rows * (v + 1), :],
+                in_=vector.rearrange("(r c) -> r c", c=P),
+            )
+
+        with tc.tile_pool(name="front", bufs=1) as front:
+            ft_sb = front.tile([P, C_TXT], BF16)
+            nc.sync.dma_start(out=ft_sb[:], in_=ft)
+            wfc = front.tile([P, rows, C_TXT], BF16)
+            wfc_dram = Wfc1.rearrange("(r p) k -> p r k", p=P)
+            for r in range(rows):
+                nc.sync.dma_start(out=wfc[:, r, :], in_=wfc_dram[:, r, :])
+            fv_sb = front.tile([P, PASSES, chunk], BF16)
+            for g in range(PASSES):
+                nc.sync.dma_start(out=fv_sb[:, g, :], in_=fv_rows[:, chunk * g : chunk * (g + 1)])
+            nc.sync.dma_start(
+                out=w_words[:].bitcast(I32),
+                in_=W1_words.rearrange("g p n -> p g n").bitcast(I32),
+            )
+            for quad in range(4):
+                nc.sync.dma_start(
+                    out=w_scales[32 * quad : 32 * quad + 4].bitcast(I32),
+                    in_=W1_scales[:, 4 * quad : 4 * quad + 4, :].rearrange("g r n -> r g n").bitcast(I32),
+                )
+
+            vec_t = psum.tile([P, P], BF16, tag="bank")
+            nc.tensor.transpose(vec_t[:], vec_rows[:], ident_bf[:])
+            nc.vector.tensor_copy(
+                out=cols[:], in_=vec_t[:, 0 : len(vectors) * rows].rearrange("p (v r) -> p v r", r=rows)
+            )
+            col_b1, col_g1, col_be1, col_m1, col_v1, col_bfc1 = [cols[:, v, :] for v in range(len(vectors))]
+            nc.vector.tensor_scalar_add(out=std[:], in0=col_v1, scalar1=EPS)
+            nc.scalar.activation(out=std[:], in_=std[:], func=ACT.Sqrt)
+            nc.vector.reciprocal(out=rstd[:], in_=std[:])
+            nc.vector.tensor_mul(out=trio[:, 0, :], in0=col_g1, in1=rstd[:])
+            nc.vector.tensor_sub(out=trio[:, 1, :], in0=col_b1, in1=col_m1)
+            nc.vector.tensor_mul(out=trio[:, 1, :], in0=trio[:, 1, :], in1=trio[:, 0, :])
+            nc.vector.tensor_add(out=trio[:, 1, :], in0=trio[:, 1, :], in1=col_be1)
+            nc.vector.tensor_scalar_add(out=trio[:, 2, :], in0=col_bfc1, scalar1=1.0)
+            repeated = front.tile([P, 3 * rows, P], F32)
+            nc.vector.tensor_copy(
+                out=repeated[:],
+                in_=trio[:].rearrange("p v r -> p (v r)").unsqueeze(2).to_broadcast([P, 3 * rows, P]),
+            )
+            per_bank = N_TILE // P
+            for v in range(3):
+                for half in range(HALVES):
+                    spread_t = psum.tile([P, per_bank, P], F32, tag="bank")
+                    for q in range(per_bank):
+                        nc.tensor.transpose(
+                            spread_t[:, q, :], repeated[:, rows * v + per_bank * half + q, :], ident_f32[:]
+                        )
+                    nc.vector.tensor_copy(
+                        out=spread[:, v, N_TILE * half : N_TILE * (half + 1)],
+                        in_=spread_t[:].rearrange("b q o -> b (q o)"),
+                    )
+
+            ft_t = psum.tile([P, k_tiles, P], BF16, tag="bank")
+            for kt in range(k_tiles):
+                nc.tensor.transpose(ft_t[:, kt, :], ft_sb[:, P * kt : P * (kt + 1)], ident_bf[:])
+            nc.scalar.copy(out=ftT[:], in_=ft_t[:])
+            for r in range(rows):
+                wfc_t = psum.tile([P, k_tiles, P], BF16, tag="bank")
+                for kt in range(k_tiles):
+                    nc.tensor.transpose(wfc_t[:, kt, :], wfc[:, r, P * kt : P * (kt + 1)], ident_bf[:])
+                nc.scalar.copy(out=wfcT[:, :, P * r : P * (r + 1)], in_=wfc_t[:])
+            for half in range(HALVES):
+                o_cols = slice(N_TILE * half, N_TILE * (half + 1))
+                gate_acc = psum.tile([P, N_TILE], F32, tag="bank")
+                for kt in range(k_tiles):
+                    nc.tensor.matmul(
+                        out=gate_acc[:],
+                        lhsT=ftT[:, kt, :],
+                        rhs=wfcT[:, kt, o_cols],
+                        start=(kt == 0),
+                        stop=(kt == k_tiles - 1),
+                    )
+                nc.vector.tensor_add(out=gate[:, o_cols], in0=gate_acc[:], in1=spread[:, 2, o_cols])
+
+            odd_bufs = 3
+            odd_tiles = [front.tile([P, (K_PASS // 2) * ODD_PITCH], BF16, name="odd%d" % i) for i in range(odd_bufs)]
+            for odd in odd_tiles:
+                nc.vector.memset(odd[:], 0.0)
+            with tc.tile_pool(name="regroup", bufs=4) as regroup:
+                for g in range(PASSES):
+                    odd = odd_tiles[g % odd_bufs]
+                    nc.vector.tensor_copy(
+                        out=odd[:].rearrange("b (c x) -> b c x", x=ODD_PITCH)[:, :, 0:PIX],
+                        in_=fv_sb[:, g, :].rearrange("b (c two x) -> b c two x", two=2, x=PIX)[:, :, 1, :],
+                    )
+                    even_words = fv_sb[:, g, :].bitcast(F32).rearrange("b (p w) -> b p w", p=P)
+                    odd_words = odd[:].bitcast(F32).rearrange("b (p w) -> b p w", p=P)
+                    for pair in range(PAIRS):
+                        n_pix = min(2, PIX - 2 * pair)
+                        planes = psum.tile([P, PACK, P], F32, tag="bank")
+                        for t in range(PACK):
+                            if t % 2 == 0:
+                                words = even_words[:, :, PIX * (t // 2) + pair]
+                            else:
+                                words = odd_words[:, :, PAIRS * (t // 2) + pair]
+                            nc.tensor.transpose(planes[:, t, :], words, ident_f32[:])
+                        grouped = regroup.tile([P, 2, P, PACK], BF16, align_bytes=64)
+                        by_pixel = (
+                            planes[:]
+                            .rearrange("p t b -> p (t b)")
+                            .bitcast(BF16)
+                            .rearrange("p (t b e) -> p e b t", t=PACK, e=2)
+                        )
+                        if n_pix == 2:
+                            nc.scalar.copy(out=grouped[:], in_=by_pixel)
+                        else:
+                            nc.vector.tensor_copy(out=grouped[:, 0:n_pix], in_=by_pixel[:, 0:n_pix])
+                        cols_q = slice(2 * P * pair, 2 * P * pair + P * n_pix)
+                        nc.vector.quantize_mx(
+                            out=fv_codes[:, g, cols_q].bitcast(FP8X4),
+                            scales=fv_scales[:, g, cols_q],
+                            in_=grouped[:, 0:n_pix].rearrange("p e b t -> p (e b t)"),
+                        )
+
+        with tc.tile_pool(name="planes", bufs=2) as plane_pool, tc.tile_pool(name="store", bufs=4) as store_pool:
+            for half in range(HALVES):
+                o_cols = slice(N_TILE * half, N_TILE * (half + 1))
+                normed = plane_pool.tile([P, PIX, N_TILE], F32)
+                for pix in range(PIX):
+                    b_cols = slice(P * pix, P * (pix + 1))
+                    acc = psum.tile([P, N_TILE], F32, tag="bank")
+                    for g in range(PASSES):
+                        nc.tensor.matmul_mx(
+                            out=acc[:],
+                            lhsT=fv_codes[:, g, b_cols].bitcast(FP8X4),
+                            lhsT_scale=fv_scales[:, g, b_cols],
+                            rhs=w_words[:, g, 2 * N_TILE * half : 2 * N_TILE * (half + 1)].bitcast(FP4X4),
+                            rhs_scale=w_scales[:, g, o_cols],
+                            start=(g == 0),
+                            stop=(g == PASSES - 1),
+                        )
+                    nc.vector.tensor_mul(out=normed[:, pix, :], in0=acc[:], in1=spread[:, 0, o_cols])
+                    nc.vector.tensor_add(out=normed[:, pix, :], in0=normed[:, pix, :], in1=spread[:, 1, o_cols])
+                for piece in range(N_TILE // O_STORE):
+                    o_lo = O_STORE * piece
+                    o_abs = N_TILE * half + o_lo
+                    result = store_pool.tile([P, O_STORE, PIX], F32)
+                    nc.vector.scalar_tensor_tensor(
+                        out=result[:],
+                        in0=normed[:, :, o_lo : o_lo + O_STORE].rearrange("b x o -> b o x"),
+                        scalar=0.0,
+                        in1=gate[:, o_abs : o_abs + O_STORE].unsqueeze(2).to_broadcast([P, O_STORE, PIX]),
+                        op0=ALU.max,
+                        op1=ALU.mult,
+                    )
+                    nc.sync.dma_start(
+                        out=out_rows[:, PIX * o_abs : PIX * (o_abs + O_STORE)],
+                        in_=result[:].rearrange("b o x -> b (o x)"),
+                    )

@@ -22,11 +22,12 @@ EPS = 1e-5
 PACK = 4
 K_PASS = P * PACK
 PASSES = C_IN // K_PASS
-N_TILE = 512
-HALVES = C_OUT // N_TILE
+BANK = 512
+HALVES = C_OUT // BANK
+N_TILE = 128
+PER_BANK = BANK // N_TILE
 PAIRS = (PIX + 1) // 2
 ODD_PITCH = 2 * PAIRS
-O_STORE = 128
 
 FLOPS = 2 * P * PIX * C_IN * C_OUT + 2 * P * C_TXT * C_OUT
 
@@ -38,16 +39,17 @@ def tile_joint_module_pa_kernel(
     fv_rows = fv.rearrange("b c h w -> b (c h w)")
     out_rows = out.rearrange("b o h w -> b (o h w)")
     chunk = K_PASS * PIX
+    vectors = [b1, g1, be1, m1, v1, bfc1]
+    rows = C_OUT // P
+    k_tiles = C_TXT // P
+    odd_bufs = 3
 
     with ExitStack() as ctx:
+        ctx.enter_context(tc.manual_schedule())
         keep = ctx.enter_context(tc.tile_pool(name="keep", bufs=1))
-        psum = ctx.enter_context(tc.psum_pool(name="psum", bufs=8))
-
-        vectors = [b1, g1, be1, m1, v1, bfc1]
-        rows = C_OUT // P
-        k_tiles = C_TXT // P
 
         w_words = keep.tile([P, PASSES, 2 * C_OUT], U8, align_bytes=64)
+        w_scales = keep.tile([P, PASSES, C_OUT], U8, align_bytes=64)
         fv_codes = keep.tile([P, PASSES, PIX * P], U32, align_bytes=64)
         fv_scales = keep.tile([P, PASSES, PIX * P], U8, align_bytes=64)
         cols = keep.tile([P, len(vectors), rows], F32)
@@ -58,31 +60,39 @@ def tile_joint_module_pa_kernel(
         ftT = keep.tile([P, k_tiles, P], BF16)
         wfcT = keep.tile([P, k_tiles, C_OUT], BF16)
         gate = keep.tile([P, C_OUT], F32)
-
         ident_bf = keep.tile([P, P], BF16)
-        make_identity(nc, ident_bf[:])
         ident_f32 = keep.tile([P, P], F32)
-        make_identity(nc, ident_f32[:])
-
+        warm = keep.tile([P, 1], F32)
         vec_rows = keep.tile([P, P], BF16)
-        nc.vector.memset(vec_rows[:], 0.0)
-        w_scales = keep.tile([P, PASSES, C_OUT], U8, align_bytes=64)
-        nc.vector.memset(w_scales[:].rearrange("p g n -> p (g n)").bitcast(I32), 0)
 
-        for v, vector in enumerate(vectors):
-            nc.scalar.dma_start(
-                out=vec_rows[rows * v : rows * (v + 1), :],
-                in_=vector.rearrange("(r c) -> r c", c=P),
-            )
-
-        with tc.tile_pool(name="front", bufs=1) as front:
+        with ExitStack() as first_part:
+            front = first_part.enter_context(tc.tile_pool(name="front", bufs=1))
+            regroup = first_part.enter_context(tc.tile_pool(name="regroup", bufs=8))
+            turn = first_part.enter_context(tc.psum_pool(name="turn", bufs=6))
+            side = first_part.enter_context(tc.psum_pool(name="side", bufs=2))
             ft_sb = front.tile([P, C_TXT], BF16)
-            nc.sync.dma_start(out=ft_sb[:], in_=ft)
             wfc = front.tile([P, rows, C_TXT], BF16)
+            fv_sb = front.tile([P, PASSES, chunk], BF16)
+            odd_tiles = [front.tile([P, (K_PASS // 2) * ODD_PITCH], BF16, name="odd%d" % i) for i in range(odd_bufs)]
+
+            make_identity(nc, ident_bf[:])
+            make_identity(nc, ident_f32[:])
+            nc.vector.memset(vec_rows[:], 0.0)
+            for v, vector in enumerate(vectors):
+                nc.scalar.dma_start(
+                    out=vec_rows[rows * v : rows * (v + 1), :],
+                    in_=vector.rearrange("(r c) -> r c", c=P),
+                )
+            nc.vector.memset(warm[:], 1.0)
+            nc.scalar.activation(out=warm[:], in_=warm[:], func=ACT.Sqrt)
+            nc.vector.memset(w_scales[:].rearrange("p g n -> p (g n)").bitcast(I32), 0)
+            for odd in odd_tiles:
+                nc.vector.memset(odd[:], 0.0)
+
+            nc.sync.dma_start(out=ft_sb[:], in_=ft)
             wfc_dram = Wfc1.rearrange("(r p) k -> p r k", p=P)
             for r in range(rows):
                 nc.sync.dma_start(out=wfc[:, r, :], in_=wfc_dram[:, r, :])
-            fv_sb = front.tile([P, PASSES, chunk], BF16)
             for g in range(PASSES):
                 nc.sync.dma_start(out=fv_sb[:, g, :], in_=fv_rows[:, chunk * g : chunk * (g + 1)])
             nc.sync.dma_start(
@@ -95,7 +105,7 @@ def tile_joint_module_pa_kernel(
                     in_=W1_scales[:, 4 * quad : 4 * quad + 4, :].rearrange("g r n -> r g n").bitcast(I32),
                 )
 
-            vec_t = psum.tile([P, P], BF16, tag="bank")
+            vec_t = side.tile([P, P], BF16, tag="bank")
             nc.tensor.transpose(vec_t[:], vec_rows[:], ident_bf[:])
             nc.vector.tensor_copy(
                 out=cols[:], in_=vec_t[:, 0 : len(vectors) * rows].rearrange("p (v r) -> p v r", r=rows)
@@ -109,36 +119,38 @@ def tile_joint_module_pa_kernel(
             nc.vector.tensor_mul(out=trio[:, 1, :], in0=trio[:, 1, :], in1=trio[:, 0, :])
             nc.vector.tensor_add(out=trio[:, 1, :], in0=trio[:, 1, :], in1=col_be1)
             nc.vector.tensor_scalar_add(out=trio[:, 2, :], in0=col_bfc1, scalar1=1.0)
-            repeated = front.tile([P, 3 * rows, P], F32)
-            nc.vector.tensor_copy(
-                out=repeated[:],
-                in_=trio[:].rearrange("p v r -> p (v r)").unsqueeze(2).to_broadcast([P, 3 * rows, P]),
-            )
-            per_bank = N_TILE // P
-            for v in range(3):
-                for half in range(HALVES):
-                    spread_t = psum.tile([P, per_bank, P], F32, tag="bank")
-                    for q in range(per_bank):
-                        nc.tensor.transpose(
-                            spread_t[:, q, :], repeated[:, rows * v + per_bank * half + q, :], ident_f32[:]
-                        )
-                    nc.vector.tensor_copy(
-                        out=spread[:, v, N_TILE * half : N_TILE * (half + 1)],
-                        in_=spread_t[:].rearrange("b q o -> b (q o)"),
-                    )
 
-            ft_t = psum.tile([P, k_tiles, P], BF16, tag="bank")
+            ft_t = turn.tile([P, k_tiles, P], BF16, tag="bank")
             for kt in range(k_tiles):
                 nc.tensor.transpose(ft_t[:, kt, :], ft_sb[:, P * kt : P * (kt + 1)], ident_bf[:])
             nc.scalar.copy(out=ftT[:], in_=ft_t[:])
             for r in range(rows):
-                wfc_t = psum.tile([P, k_tiles, P], BF16, tag="bank")
+                wfc_t = turn.tile([P, k_tiles, P], BF16, tag="bank")
                 for kt in range(k_tiles):
                     nc.tensor.transpose(wfc_t[:, kt, :], wfc[:, r, P * kt : P * (kt + 1)], ident_bf[:])
                 nc.scalar.copy(out=wfcT[:, :, P * r : P * (r + 1)], in_=wfc_t[:])
-            for half in range(HALVES):
-                o_cols = slice(N_TILE * half, N_TILE * (half + 1))
-                gate_acc = psum.tile([P, N_TILE], F32, tag="bank")
+
+            per_bank = BANK // P
+            for v in range(3):
+                for half in range(HALVES):
+                    spread_t = side.tile([P, per_bank, P], F32, tag="bank")
+                    for q in range(per_bank):
+                        r = per_bank * half + q
+                        nc.tensor.transpose(spread_t[:, q, :], trio[:, v, r : r + 1].to_broadcast([P, P]), ident_f32[:])
+                    nc.scalar.copy(
+                        out=spread[:, v, BANK * half : BANK * (half + 1)],
+                        in_=spread_t[:].rearrange("b q o -> b (q o)"),
+                    )
+
+            def realign_odd_channels(g):
+                nc.vector.tensor_copy(
+                    out=odd_tiles[g % odd_bufs][:].rearrange("b (c x) -> b c x", x=ODD_PITCH)[:, :, 0:PIX],
+                    in_=fv_sb[:, g, :].rearrange("b (c two x) -> b c two x", two=2, x=PIX)[:, :, 1, :],
+                )
+
+            def gate_half(half):
+                o_cols = slice(BANK * half, BANK * (half + 1))
+                gate_acc = side.tile([P, BANK], F32, tag="bank")
                 for kt in range(k_tiles):
                     nc.tensor.matmul(
                         out=gate_acc[:],
@@ -149,78 +161,97 @@ def tile_joint_module_pa_kernel(
                     )
                 nc.vector.tensor_add(out=gate[:, o_cols], in0=gate_acc[:], in1=spread[:, 2, o_cols])
 
-            odd_bufs = 3
-            odd_tiles = [front.tile([P, (K_PASS // 2) * ODD_PITCH], BF16, name="odd%d" % i) for i in range(odd_bufs)]
-            for odd in odd_tiles:
-                nc.vector.memset(odd[:], 0.0)
-            with tc.tile_pool(name="regroup", bufs=4) as regroup:
-                for g in range(PASSES):
-                    odd = odd_tiles[g % odd_bufs]
-                    nc.vector.tensor_copy(
-                        out=odd[:].rearrange("b (c x) -> b c x", x=ODD_PITCH)[:, :, 0:PIX],
-                        in_=fv_sb[:, g, :].rearrange("b (c two x) -> b c two x", two=2, x=PIX)[:, :, 1, :],
-                    )
-                    even_words = fv_sb[:, g, :].bitcast(F32).rearrange("b (p w) -> b p w", p=P)
-                    odd_words = odd[:].bitcast(F32).rearrange("b (p w) -> b p w", p=P)
-                    for pair in range(PAIRS):
-                        n_pix = min(2, PIX - 2 * pair)
-                        planes = psum.tile([P, PACK, P], F32, tag="bank")
-                        for t in range(PACK):
-                            if t % 2 == 0:
-                                words = even_words[:, :, PIX * (t // 2) + pair]
-                            else:
-                                words = odd_words[:, :, PAIRS * (t // 2) + pair]
-                            nc.tensor.transpose(planes[:, t, :], words, ident_f32[:])
-                        grouped = regroup.tile([P, 2, P, PACK], BF16, align_bytes=64)
-                        by_pixel = (
-                            planes[:]
-                            .rearrange("p t b -> p (t b)")
-                            .bitcast(BF16)
-                            .rearrange("p (t b e) -> p e b t", t=PACK, e=2)
-                        )
-                        if n_pix == 2:
-                            nc.scalar.copy(out=grouped[:], in_=by_pixel)
+            realign_odd_channels(0)
+            for g in range(PASSES):
+                if g + 1 < PASSES:
+                    realign_odd_channels(g + 1)
+                even_words = fv_sb[:, g, :].bitcast(F32).rearrange("b (p w) -> b p w", p=P)
+                odd_words = odd_tiles[g % odd_bufs][:].bitcast(F32).rearrange("b (p w) -> b p w", p=P)
+                grouped_tiles = []
+                for pair in range(PAIRS):
+                    n_pix = min(2, PIX - 2 * pair)
+                    planes = turn.tile([P, PACK, P], F32, tag="bank")
+                    for t in range(PACK):
+                        if t % 2 == 0:
+                            words = even_words[:, :, PIX * (t // 2) + pair]
                         else:
-                            nc.vector.tensor_copy(out=grouped[:, 0:n_pix], in_=by_pixel[:, 0:n_pix])
-                        cols_q = slice(2 * P * pair, 2 * P * pair + P * n_pix)
-                        nc.vector.quantize_mx(
-                            out=fv_codes[:, g, cols_q].bitcast(FP8X4),
-                            scales=fv_scales[:, g, cols_q],
-                            in_=grouped[:, 0:n_pix].rearrange("p e b t -> p (e b t)"),
-                        )
+                            words = odd_words[:, :, PAIRS * (t // 2) + pair]
+                        nc.tensor.transpose(planes[:, t, :], words, ident_f32[:])
+                    grouped = regroup.tile([P, 2, P, PACK], BF16, align_bytes=64)
+                    by_pixel = (
+                        planes[:]
+                        .rearrange("p t b -> p (t b)")
+                        .bitcast(BF16)
+                        .rearrange("p (t b e) -> p e b t", t=PACK, e=2)
+                    )
+                    if pair < PAIRS - 2 or (pair == PAIRS - 2 and g % 2 == 0):
+                        nc.scalar.copy(out=grouped[:], in_=by_pixel)
+                    else:
+                        nc.vector.tensor_copy(out=grouped[:, 0:n_pix], in_=by_pixel[:, 0:n_pix])
+                    grouped_tiles.append(grouped)
+                if g < HALVES:
+                    gate_half(g)
+                for pair in range(PAIRS):
+                    n_pix = min(2, PIX - 2 * pair)
+                    cols_q = slice(2 * P * pair, 2 * P * pair + P * n_pix)
+                    nc.vector.quantize_mx(
+                        out=fv_codes[:, g, cols_q].bitcast(FP8X4),
+                        scales=fv_scales[:, g, cols_q],
+                        in_=grouped_tiles[pair][:, 0:n_pix].rearrange("p e b t -> p (e b t)"),
+                    )
 
-        with tc.tile_pool(name="planes", bufs=2) as plane_pool, tc.tile_pool(name="store", bufs=4) as store_pool:
-            for half in range(HALVES):
-                o_cols = slice(N_TILE * half, N_TILE * (half + 1))
+        with ExitStack() as second_part:
+            plane_pool = second_part.enter_context(tc.tile_pool(name="planes", bufs=3))
+            store_pool = second_part.enter_context(tc.tile_pool(name="store", bufs=3))
+            psum = second_part.enter_context(tc.psum_pool(name="psum", bufs=8))
+
+            def finish(o_tile, normed):
+                o_cols = slice(N_TILE * o_tile, N_TILE * (o_tile + 1))
+                result = store_pool.tile([P, N_TILE, PIX], F32)
+                nc.vector.scalar_tensor_tensor(
+                    out=result[:],
+                    in0=normed[:].rearrange("b x o -> b o x"),
+                    scalar=0.0,
+                    in1=gate[:, o_cols].unsqueeze(2).to_broadcast([P, N_TILE, PIX]),
+                    op0=ALU.max,
+                    op1=ALU.mult,
+                )
+                nc.sync.dma_start(
+                    out=out_rows[:, PIX * N_TILE * o_tile : PIX * N_TILE * (o_tile + 1)],
+                    in_=result[:].rearrange("b o x -> b (o x)"),
+                )
+
+            previous = None
+            for o_tile in range(C_OUT // N_TILE):
+                o_cols = slice(N_TILE * o_tile, N_TILE * (o_tile + 1))
                 normed = plane_pool.tile([P, PIX, N_TILE], F32)
-                for pix in range(PIX):
-                    b_cols = slice(P * pix, P * (pix + 1))
-                    acc = psum.tile([P, N_TILE], F32, tag="bank")
-                    for g in range(PASSES):
-                        nc.tensor.matmul_mx(
-                            out=acc[:],
-                            lhsT=fv_codes[:, g, b_cols].bitcast(FP8X4),
-                            lhsT_scale=fv_scales[:, g, b_cols],
-                            rhs=w_words[:, g, 2 * N_TILE * half : 2 * N_TILE * (half + 1)].bitcast(FP4X4),
-                            rhs_scale=w_scales[:, g, o_cols],
-                            start=(g == 0),
-                            stop=(g == PASSES - 1),
-                        )
-                    nc.vector.tensor_mul(out=normed[:, pix, :], in0=acc[:], in1=spread[:, 0, o_cols])
-                    nc.vector.tensor_add(out=normed[:, pix, :], in0=normed[:, pix, :], in1=spread[:, 1, o_cols])
-                for piece in range(N_TILE // O_STORE):
-                    o_lo = O_STORE * piece
-                    o_abs = N_TILE * half + o_lo
-                    result = store_pool.tile([P, O_STORE, PIX], F32)
-                    nc.vector.scalar_tensor_tensor(
-                        out=result[:],
-                        in0=normed[:, :, o_lo : o_lo + O_STORE].rearrange("b x o -> b o x"),
-                        scalar=0.0,
-                        in1=gate[:, o_abs : o_abs + O_STORE].unsqueeze(2).to_broadcast([P, O_STORE, PIX]),
-                        op0=ALU.max,
-                        op1=ALU.mult,
+                for first in range(0, PIX, PER_BANK):
+                    n_pix = min(PER_BANK, PIX - first)
+                    acc = psum.tile([P, PER_BANK, N_TILE], F32, tag="bank")
+                    for i in range(n_pix):
+                        b_cols = slice(P * (first + i), P * (first + i + 1))
+                        for g in range(PASSES):
+                            nc.tensor.matmul_mx(
+                                out=acc[:, i, :],
+                                lhsT=fv_codes[:, g, b_cols].bitcast(FP8X4),
+                                lhsT_scale=fv_scales[:, g, b_cols],
+                                rhs=w_words[:, g, 2 * N_TILE * o_tile : 2 * N_TILE * (o_tile + 1)].bitcast(FP4X4),
+                                rhs_scale=w_scales[:, g, o_cols],
+                                start=(g == 0),
+                                stop=(g == PASSES - 1),
+                            )
+                    block = normed[:, first : first + n_pix, :]
+                    nc.vector.tensor_mul(
+                        out=block,
+                        in0=acc[:, 0:n_pix, :],
+                        in1=spread[:, 0, o_cols].unsqueeze(1).to_broadcast([P, n_pix, N_TILE]),
                     )
-                    nc.sync.dma_start(
-                        out=out_rows[:, PIX * o_abs : PIX * (o_abs + O_STORE)],
-                        in_=result[:].rearrange("b o x -> b (o x)"),
+                    nc.vector.tensor_add(
+                        out=block,
+                        in0=block,
+                        in1=spread[:, 1, o_cols].unsqueeze(1).to_broadcast([P, n_pix, N_TILE]),
                     )
+                    if first == 0 and previous is not None:
+                        finish(o_tile - 1, previous)
+                previous = normed
+            finish(C_OUT // N_TILE - 1, previous)

@@ -39,17 +39,16 @@ def tile_joint_module_pa_kernel(
     fv_rows = fv.rearrange("b c h w -> b (c h w)")
     out_rows = out.rearrange("b o h w -> b (o h w)")
     chunk = K_PASS * PIX
-    vectors = [b1, g1, be1, m1, v1, bfc1]
-    rows = C_OUT // P
-    k_tiles = C_TXT // P
-    odd_bufs = 3
 
     with ExitStack() as ctx:
-        ctx.enter_context(tc.manual_schedule())
         keep = ctx.enter_context(tc.tile_pool(name="keep", bufs=1))
+        psum = ctx.enter_context(tc.psum_pool(name="psum", bufs=8))
+
+        vectors = [b1, g1, be1, m1, v1, bfc1]
+        rows = C_OUT // P
+        k_tiles = C_TXT // P
 
         w_words = keep.tile([P, PASSES, 2 * C_OUT], U8, align_bytes=64)
-        w_scales = keep.tile([P, PASSES, C_OUT], U8, align_bytes=64)
         fv_codes = keep.tile([P, PASSES, PIX * P], U32, align_bytes=64)
         fv_scales = keep.tile([P, PASSES, PIX * P], U8, align_bytes=64)
         cols = keep.tile([P, len(vectors), rows], F32)
@@ -60,39 +59,35 @@ def tile_joint_module_pa_kernel(
         ftT = keep.tile([P, k_tiles, P], BF16)
         wfcT = keep.tile([P, k_tiles, C_OUT], BF16)
         gate = keep.tile([P, C_OUT], F32)
+
         ident_bf = keep.tile([P, P], BF16)
+        make_identity(nc, ident_bf[:])
         ident_f32 = keep.tile([P, P], F32)
+        make_identity(nc, ident_f32[:])
+
         warm = keep.tile([P, 1], F32)
+        nc.vector.memset(warm[:], 1.0)
+        nc.scalar.activation(out=warm[:], in_=warm[:], func=ACT.Sqrt)
+
         vec_rows = keep.tile([P, P], BF16)
+        nc.vector.memset(vec_rows[:], 0.0)
+        w_scales = keep.tile([P, PASSES, C_OUT], U8, align_bytes=64)
+        nc.vector.memset(w_scales[:].rearrange("p g n -> p (g n)").bitcast(I32), 0)
 
-        with ExitStack() as first_part:
-            front = first_part.enter_context(tc.tile_pool(name="front", bufs=1))
-            regroup = first_part.enter_context(tc.tile_pool(name="regroup", bufs=8))
-            turn = first_part.enter_context(tc.psum_pool(name="turn", bufs=6))
-            side = first_part.enter_context(tc.psum_pool(name="side", bufs=2))
+        for v, vector in enumerate(vectors):
+            nc.sync.dma_start(
+                out=vec_rows[rows * v : rows * (v + 1), :],
+                in_=vector.rearrange("(r c) -> r c", c=P),
+            )
+
+        with tc.tile_pool(name="front", bufs=1) as front:
             ft_sb = front.tile([P, C_TXT], BF16)
-            wfc = front.tile([P, rows, C_TXT], BF16)
-            fv_sb = front.tile([P, PASSES, chunk], BF16)
-            odd_tiles = [front.tile([P, (K_PASS // 2) * ODD_PITCH], BF16, name="odd%d" % i) for i in range(odd_bufs)]
-
-            make_identity(nc, ident_bf[:])
-            make_identity(nc, ident_f32[:])
-            nc.vector.memset(vec_rows[:], 0.0)
-            for v, vector in enumerate(vectors):
-                nc.scalar.dma_start(
-                    out=vec_rows[rows * v : rows * (v + 1), :],
-                    in_=vector.rearrange("(r c) -> r c", c=P),
-                )
-            nc.vector.memset(warm[:], 1.0)
-            nc.scalar.activation(out=warm[:], in_=warm[:], func=ACT.Sqrt)
-            nc.vector.memset(w_scales[:].rearrange("p g n -> p (g n)").bitcast(I32), 0)
-            for odd in odd_tiles:
-                nc.vector.memset(odd[:], 0.0)
-
             nc.sync.dma_start(out=ft_sb[:], in_=ft)
+            wfc = front.tile([P, rows, C_TXT], BF16)
             wfc_dram = Wfc1.rearrange("(r p) k -> p r k", p=P)
             for r in range(rows):
                 nc.sync.dma_start(out=wfc[:, r, :], in_=wfc_dram[:, r, :])
+            fv_sb = front.tile([P, PASSES, chunk], BF16)
             for g in range(PASSES):
                 nc.sync.dma_start(out=fv_sb[:, g, :], in_=fv_rows[:, chunk * g : chunk * (g + 1)])
             nc.sync.dma_start(
@@ -105,7 +100,7 @@ def tile_joint_module_pa_kernel(
                     in_=W1_scales[:, 4 * quad : 4 * quad + 4, :].rearrange("g r n -> r g n").bitcast(I32),
                 )
 
-            vec_t = side.tile([P, P], BF16, tag="bank")
+            vec_t = psum.tile([P, P], BF16, tag="bank")
             nc.tensor.transpose(vec_t[:], vec_rows[:], ident_bf[:])
             nc.vector.tensor_copy(
                 out=cols[:], in_=vec_t[:, 0 : len(vectors) * rows].rearrange("p (v r) -> p v r", r=rows)
@@ -119,13 +114,12 @@ def tile_joint_module_pa_kernel(
             nc.vector.tensor_mul(out=trio[:, 1, :], in0=trio[:, 1, :], in1=trio[:, 0, :])
             nc.vector.tensor_add(out=trio[:, 1, :], in0=trio[:, 1, :], in1=col_be1)
             nc.vector.tensor_scalar_add(out=trio[:, 2, :], in0=col_bfc1, scalar1=1.0)
-
-            ft_t = turn.tile([P, k_tiles, P], BF16, tag="bank")
+            ft_t = psum.tile([P, k_tiles, P], BF16, tag="bank")
             for kt in range(k_tiles):
                 nc.tensor.transpose(ft_t[:, kt, :], ft_sb[:, P * kt : P * (kt + 1)], ident_bf[:])
             nc.scalar.copy(out=ftT[:], in_=ft_t[:])
             for r in range(rows):
-                wfc_t = turn.tile([P, k_tiles, P], BF16, tag="bank")
+                wfc_t = psum.tile([P, k_tiles, P], BF16, tag="bank")
                 for kt in range(k_tiles):
                     nc.tensor.transpose(wfc_t[:, kt, :], wfc[:, r, P * kt : P * (kt + 1)], ident_bf[:])
                 nc.scalar.copy(out=wfcT[:, :, P * r : P * (r + 1)], in_=wfc_t[:])
@@ -133,77 +127,72 @@ def tile_joint_module_pa_kernel(
             per_bank = BANK // P
             for v in range(3):
                 for half in range(HALVES):
-                    spread_t = side.tile([P, per_bank, P], F32, tag="bank")
+                    spread_t = psum.tile([P, per_bank, P], F32, tag="bank")
                     for q in range(per_bank):
                         r = per_bank * half + q
                         nc.tensor.transpose(spread_t[:, q, :], trio[:, v, r : r + 1].to_broadcast([P, P]), ident_f32[:])
-                    nc.scalar.copy(
+                    nc.vector.tensor_copy(
                         out=spread[:, v, BANK * half : BANK * (half + 1)],
                         in_=spread_t[:].rearrange("b q o -> b (q o)"),
                     )
 
-            def realign_odd_channels(g):
-                nc.vector.tensor_copy(
-                    out=odd_tiles[g % odd_bufs][:].rearrange("b (c x) -> b c x", x=ODD_PITCH)[:, :, 0:PIX],
-                    in_=fv_sb[:, g, :].rearrange("b (c two x) -> b c two x", two=2, x=PIX)[:, :, 1, :],
-                )
-
-            def gate_half(half):
-                o_cols = slice(BANK * half, BANK * (half + 1))
-                gate_acc = side.tile([P, BANK], F32, tag="bank")
-                for kt in range(k_tiles):
-                    nc.tensor.matmul(
-                        out=gate_acc[:],
-                        lhsT=ftT[:, kt, :],
-                        rhs=wfcT[:, kt, o_cols],
-                        start=(kt == 0),
-                        stop=(kt == k_tiles - 1),
+            odd_bufs = 3
+            odd_tiles = [front.tile([P, (K_PASS // 2) * ODD_PITCH], BF16, name="odd%d" % i) for i in range(odd_bufs)]
+            for odd in odd_tiles:
+                nc.vector.memset(odd[:], 0.0)
+            with tc.tile_pool(name="regroup", bufs=4) as regroup:
+                for g in range(PASSES):
+                    odd = odd_tiles[g % odd_bufs]
+                    nc.vector.tensor_copy(
+                        out=odd[:].rearrange("b (c x) -> b c x", x=ODD_PITCH)[:, :, 0:PIX],
+                        in_=fv_sb[:, g, :].rearrange("b (c two x) -> b c two x", two=2, x=PIX)[:, :, 1, :],
                     )
-                nc.vector.tensor_add(out=gate[:, o_cols], in0=gate_acc[:], in1=spread[:, 2, o_cols])
-
-            realign_odd_channels(0)
-            for g in range(PASSES):
-                if g + 1 < PASSES:
-                    realign_odd_channels(g + 1)
-                even_words = fv_sb[:, g, :].bitcast(F32).rearrange("b (p w) -> b p w", p=P)
-                odd_words = odd_tiles[g % odd_bufs][:].bitcast(F32).rearrange("b (p w) -> b p w", p=P)
-                grouped_tiles = []
-                for pair in range(PAIRS):
-                    n_pix = min(2, PIX - 2 * pair)
-                    planes = turn.tile([P, PACK, P], F32, tag="bank")
-                    for t in range(PACK):
-                        if t % 2 == 0:
-                            words = even_words[:, :, PIX * (t // 2) + pair]
+                    even_words = fv_sb[:, g, :].bitcast(F32).rearrange("b (p w) -> b p w", p=P)
+                    odd_words = odd[:].bitcast(F32).rearrange("b (p w) -> b p w", p=P)
+                    for pair in range(PAIRS):
+                        n_pix = min(2, PIX - 2 * pair)
+                        planes = psum.tile([P, PACK, P], F32, tag="bank")
+                        for t in range(PACK):
+                            if t % 2 == 0:
+                                words = even_words[:, :, PIX * (t // 2) + pair]
+                            else:
+                                words = odd_words[:, :, PAIRS * (t // 2) + pair]
+                            nc.tensor.transpose(planes[:, t, :], words, ident_f32[:])
+                        grouped = regroup.tile([P, 2, P, PACK], BF16, align_bytes=64)
+                        by_pixel = (
+                            planes[:]
+                            .rearrange("p t b -> p (t b)")
+                            .bitcast(BF16)
+                            .rearrange("p (t b e) -> p e b t", t=PACK, e=2)
+                        )
+                        if pair < PAIRS - 2 or (pair == PAIRS - 2 and g % 2 == 0):
+                            nc.scalar.copy(out=grouped[:], in_=by_pixel)
                         else:
-                            words = odd_words[:, :, PAIRS * (t // 2) + pair]
-                        nc.tensor.transpose(planes[:, t, :], words, ident_f32[:])
-                    grouped = regroup.tile([P, 2, P, PACK], BF16, align_bytes=64)
-                    by_pixel = (
-                        planes[:]
-                        .rearrange("p t b -> p (t b)")
-                        .bitcast(BF16)
-                        .rearrange("p (t b e) -> p e b t", t=PACK, e=2)
-                    )
-                    if pair < PAIRS - 2 or (pair == PAIRS - 2 and g % 2 == 0):
-                        nc.scalar.copy(out=grouped[:], in_=by_pixel)
-                    else:
-                        nc.vector.tensor_copy(out=grouped[:, 0:n_pix], in_=by_pixel[:, 0:n_pix])
-                    grouped_tiles.append(grouped)
-                if g < HALVES:
-                    gate_half(g)
-                for pair in range(PAIRS):
-                    n_pix = min(2, PIX - 2 * pair)
-                    cols_q = slice(2 * P * pair, 2 * P * pair + P * n_pix)
-                    nc.vector.quantize_mx(
-                        out=fv_codes[:, g, cols_q].bitcast(FP8X4),
-                        scales=fv_scales[:, g, cols_q],
-                        in_=grouped_tiles[pair][:, 0:n_pix].rearrange("p e b t -> p (e b t)"),
-                    )
+                            nc.vector.tensor_copy(out=grouped[:, 0:n_pix], in_=by_pixel[:, 0:n_pix])
+                        cols_q = slice(2 * P * pair, 2 * P * pair + P * n_pix)
+                        nc.vector.quantize_mx(
+                            out=fv_codes[:, g, cols_q].bitcast(FP8X4),
+                            scales=fv_scales[:, g, cols_q],
+                            in_=grouped[:, 0:n_pix].rearrange("p e b t -> p (e b t)"),
+                        )
+
+        for half in range(HALVES):
+            o_cols = slice(BANK * half, BANK * (half + 1))
+            gate_acc = psum.tile([P, BANK], F32, tag="bank")
+            for kt in range(k_tiles):
+                nc.tensor.matmul(
+                    out=gate_acc[:],
+                    lhsT=ftT[:, kt, :],
+                    rhs=wfcT[:, kt, o_cols],
+                    start=(kt == 0),
+                    stop=(kt == k_tiles - 1),
+                )
+            nc.vector.tensor_add(out=gate[:, o_cols], in0=gate_acc[:], in1=spread[:, 2, o_cols])
 
         with ExitStack() as second_part:
+            second_part.enter_context(tc.manual_schedule())
             plane_pool = second_part.enter_context(tc.tile_pool(name="planes", bufs=3))
             store_pool = second_part.enter_context(tc.tile_pool(name="store", bufs=3))
-            psum = second_part.enter_context(tc.psum_pool(name="psum", bufs=8))
 
             def finish(o_tile, normed):
                 o_cols = slice(N_TILE * o_tile, N_TILE * (o_tile + 1))
@@ -246,11 +235,11 @@ def tile_joint_module_pa_kernel(
                         in0=acc[:, 0:n_pix, :],
                         in1=spread[:, 0, o_cols].unsqueeze(1).to_broadcast([P, n_pix, N_TILE]),
                     )
-                    nc.vector.tensor_add(
-                        out=block,
-                        in0=block,
-                        in1=spread[:, 1, o_cols].unsqueeze(1).to_broadcast([P, n_pix, N_TILE]),
-                    )
+                    shift = spread[:, 1, o_cols].unsqueeze(1).to_broadcast([P, n_pix, N_TILE])
+                    if n_pix == PER_BANK:
+                        nc.gpsimd.tensor_add(out=block, in0=block, in1=shift)
+                    else:
+                        nc.vector.tensor_add(out=block, in0=block, in1=shift)
                     if first == 0 and previous is not None:
                         finish(o_tile - 1, previous)
                 previous = normed

@@ -44,7 +44,7 @@ def tile_joint_module_pa_kernel(
         keep = ctx.enter_context(tc.tile_pool(name="keep", bufs=1))
         psum = ctx.enter_context(tc.psum_pool(name="psum", bufs=8))
 
-        vectors = [b1, g1, be1, m1, v1, bfc1]
+        vectors = [b1, g1, be1, m1, v1]
         rows = C_OUT // P
         k_tiles = C_TXT // P
 
@@ -54,8 +54,8 @@ def tile_joint_module_pa_kernel(
         cols = keep.tile([P, len(vectors), rows], F32)
         std = keep.tile([P, rows], F32)
         rstd = keep.tile([P, rows], F32)
-        trio = keep.tile([P, 3, rows], F32)
-        spread = keep.tile([P, 3, C_OUT], F32)
+        duo = keep.tile([P, 2, rows], F32)
+        spread = keep.tile([P, 2, C_OUT], F32)
         ftT = keep.tile([P, k_tiles, P], BF16)
         wfcT = keep.tile([P, k_tiles, C_OUT], BF16)
         gate = keep.tile([P, C_OUT], F32)
@@ -73,6 +73,12 @@ def tile_joint_module_pa_kernel(
         nc.vector.memset(vec_rows[:], 0.0)
         w_scales = keep.tile([P, PASSES, C_OUT], U8, align_bytes=64)
         nc.vector.memset(w_scales[:].rearrange("p g n -> p (g n)").bitcast(I32), 0)
+        ones = keep.tile([P, P], BF16)
+        nc.vector.memset(ones[:], 1.0)
+        bias_rows = keep.tile([P, C_OUT], BF16)
+        nc.vector.memset(bias_rows[:], 0.0)
+        nc.vector.memset(bias_rows[0:2, :], 1.0)
+        nc.sync.dma_start(out=bias_rows[0:1, :], in_=bfc1.rearrange("(one o) -> one o", one=1))
 
         for v, vector in enumerate(vectors):
             nc.sync.dma_start(
@@ -105,32 +111,56 @@ def tile_joint_module_pa_kernel(
             nc.vector.tensor_copy(
                 out=cols[:], in_=vec_t[:, 0 : len(vectors) * rows].rearrange("p (v r) -> p v r", r=rows)
             )
-            col_b1, col_g1, col_be1, col_m1, col_v1, col_bfc1 = [cols[:, v, :] for v in range(len(vectors))]
+            col_b1, col_g1, col_be1, col_m1, col_v1 = [cols[:, v, :] for v in range(len(vectors))]
             nc.vector.tensor_scalar_add(out=std[:], in0=col_v1, scalar1=EPS)
             nc.scalar.activation(out=std[:], in_=std[:], func=ACT.Sqrt)
             nc.vector.reciprocal(out=rstd[:], in_=std[:])
-            nc.vector.tensor_mul(out=trio[:, 0, :], in0=col_g1, in1=rstd[:])
-            nc.vector.tensor_sub(out=trio[:, 1, :], in0=col_b1, in1=col_m1)
-            nc.vector.tensor_mul(out=trio[:, 1, :], in0=trio[:, 1, :], in1=trio[:, 0, :])
-            nc.vector.tensor_add(out=trio[:, 1, :], in0=trio[:, 1, :], in1=col_be1)
-            nc.vector.tensor_scalar_add(out=trio[:, 2, :], in0=col_bfc1, scalar1=1.0)
+            nc.vector.tensor_mul(out=duo[:, 0, :], in0=col_g1, in1=rstd[:])
+            nc.vector.tensor_sub(out=duo[:, 1, :], in0=col_b1, in1=col_m1)
+            nc.vector.tensor_mul(out=duo[:, 1, :], in0=duo[:, 1, :], in1=duo[:, 0, :])
+            nc.vector.tensor_add(out=duo[:, 1, :], in0=duo[:, 1, :], in1=col_be1)
+
+            per_bank = BANK // P
             ft_t = psum.tile([P, k_tiles, P], BF16, tag="bank")
             for kt in range(k_tiles):
                 nc.tensor.transpose(ft_t[:, kt, :], ft_sb[:, P * kt : P * (kt + 1)], ident_bf[:])
             nc.scalar.copy(out=ftT[:], in_=ft_t[:])
-            for r in range(rows):
-                wfc_t = psum.tile([P, k_tiles, P], BF16, tag="bank")
-                for kt in range(k_tiles):
-                    nc.tensor.transpose(wfc_t[:, kt, :], wfc[:, r, P * kt : P * (kt + 1)], ident_bf[:])
-                nc.scalar.copy(out=wfcT[:, :, P * r : P * (r + 1)], in_=wfc_t[:])
+            gate_acc = None
+            for step in range(rows + 1):
+                if step < rows:
+                    r = step
+                    wfc_t = psum.tile([P, k_tiles, P], BF16, tag="bank")
+                    for kt in range(k_tiles):
+                        nc.tensor.transpose(wfc_t[:, kt, :], wfc[:, r, P * kt : P * (kt + 1)], ident_bf[:])
+                    nc.scalar.copy(out=wfcT[:, :, P * r : P * (r + 1)], in_=wfc_t[:])
+                if step > 0:
+                    r = step - 1
+                    o_cols = slice(P * r, P * (r + 1))
+                    if r % per_bank == 0:
+                        gate_acc = psum.tile([P, per_bank, P], F32, tag="bank")
+                    for kt in range(k_tiles):
+                        nc.tensor.matmul(
+                            out=gate_acc[:, r % per_bank, :],
+                            lhsT=ftT[:, kt, :],
+                            rhs=wfcT[:, kt, o_cols],
+                            start=(kt == 0),
+                            stop=False,
+                        )
+                    nc.tensor.matmul(
+                        out=gate_acc[:, r % per_bank, :], lhsT=ones[:], rhs=bias_rows[:, o_cols], start=False, stop=True
+                    )
+                    if r % per_bank == per_bank - 1:
+                        nc.scalar.copy(
+                            out=gate[:, P * (r + 1 - per_bank) : P * (r + 1)],
+                            in_=gate_acc[:].rearrange("b q o -> b (q o)"),
+                        )
 
-            per_bank = BANK // P
-            for v in range(3):
+            for v in range(2):
                 for half in range(HALVES):
                     spread_t = psum.tile([P, per_bank, P], F32, tag="bank")
                     for q in range(per_bank):
                         r = per_bank * half + q
-                        nc.tensor.transpose(spread_t[:, q, :], trio[:, v, r : r + 1].to_broadcast([P, P]), ident_f32[:])
+                        nc.tensor.transpose(spread_t[:, q, :], duo[:, v, r : r + 1].to_broadcast([P, P]), ident_f32[:])
                     nc.vector.tensor_copy(
                         out=spread[:, v, BANK * half : BANK * (half + 1)],
                         in_=spread_t[:].rearrange("b q o -> b (q o)"),
@@ -175,19 +205,6 @@ def tile_joint_module_pa_kernel(
                             scales=fv_scales[:, g, cols_q],
                             in_=grouped[:, 0:n_pix].rearrange("p e b t -> p (e b t)"),
                         )
-
-        for half in range(HALVES):
-            o_cols = slice(BANK * half, BANK * (half + 1))
-            gate_acc = psum.tile([P, BANK], F32, tag="bank")
-            for kt in range(k_tiles):
-                nc.tensor.matmul(
-                    out=gate_acc[:],
-                    lhsT=ftT[:, kt, :],
-                    rhs=wfcT[:, kt, o_cols],
-                    start=(kt == 0),
-                    stop=(kt == k_tiles - 1),
-                )
-            nc.vector.tensor_add(out=gate[:, o_cols], in0=gate_acc[:], in1=spread[:, 2, o_cols])
 
         with ExitStack() as second_part:
             second_part.enter_context(tc.manual_schedule())

@@ -22,12 +22,11 @@ EPS = 1e-5
 PACK = 4
 K_PASS = P * PACK
 PASSES = C_IN // K_PASS
-BANK = 512
-HALVES = C_OUT // BANK
-N_TILE = 128
-PER_BANK = BANK // N_TILE
+N_TILE = 512
+HALVES = C_OUT // N_TILE
 PAIRS = (PIX + 1) // 2
 ODD_PITCH = 2 * PAIRS
+O_STORE = 128
 
 FLOPS = 2 * P * PIX * C_IN * C_OUT + 2 * P * C_TXT * C_OUT
 
@@ -44,7 +43,7 @@ def tile_joint_module_pa_kernel(
         keep = ctx.enter_context(tc.tile_pool(name="keep", bufs=1))
         psum = ctx.enter_context(tc.psum_pool(name="psum", bufs=8))
 
-        vectors = [b1, g1, be1, m1, v1]
+        vectors = [b1, g1, be1, m1, v1, bfc1]
         rows = C_OUT // P
         k_tiles = C_TXT // P
 
@@ -54,8 +53,8 @@ def tile_joint_module_pa_kernel(
         cols = keep.tile([P, len(vectors), rows], F32)
         std = keep.tile([P, rows], F32)
         rstd = keep.tile([P, rows], F32)
-        duo = keep.tile([P, 2, rows], F32)
-        spread = keep.tile([P, 2, C_OUT], F32)
+        trio = keep.tile([P, 3, rows], F32)
+        spread = keep.tile([P, 3, C_OUT], F32)
         ftT = keep.tile([P, k_tiles, P], BF16)
         wfcT = keep.tile([P, k_tiles, C_OUT], BF16)
         gate = keep.tile([P, C_OUT], F32)
@@ -73,12 +72,6 @@ def tile_joint_module_pa_kernel(
         nc.vector.memset(vec_rows[:], 0.0)
         w_scales = keep.tile([P, PASSES, C_OUT], U8, align_bytes=64)
         nc.vector.memset(w_scales[:].rearrange("p g n -> p (g n)").bitcast(I32), 0)
-        ones = keep.tile([P, P], BF16)
-        nc.vector.memset(ones[:], 1.0)
-        bias_rows = keep.tile([P, C_OUT], BF16)
-        nc.vector.memset(bias_rows[:], 0.0)
-        nc.vector.memset(bias_rows[0:2, :], 1.0)
-        nc.sync.dma_start(out=bias_rows[0:1, :], in_=bfc1.rearrange("(one o) -> one o", one=1))
 
         for v, vector in enumerate(vectors):
             nc.sync.dma_start(
@@ -111,58 +104,34 @@ def tile_joint_module_pa_kernel(
             nc.vector.tensor_copy(
                 out=cols[:], in_=vec_t[:, 0 : len(vectors) * rows].rearrange("p (v r) -> p v r", r=rows)
             )
-            col_b1, col_g1, col_be1, col_m1, col_v1 = [cols[:, v, :] for v in range(len(vectors))]
+            col_b1, col_g1, col_be1, col_m1, col_v1, col_bfc1 = [cols[:, v, :] for v in range(len(vectors))]
             nc.vector.tensor_scalar_add(out=std[:], in0=col_v1, scalar1=EPS)
             nc.scalar.activation(out=std[:], in_=std[:], func=ACT.Sqrt)
             nc.vector.reciprocal(out=rstd[:], in_=std[:])
-            nc.vector.tensor_mul(out=duo[:, 0, :], in0=col_g1, in1=rstd[:])
-            nc.vector.tensor_sub(out=duo[:, 1, :], in0=col_b1, in1=col_m1)
-            nc.vector.tensor_mul(out=duo[:, 1, :], in0=duo[:, 1, :], in1=duo[:, 0, :])
-            nc.vector.tensor_add(out=duo[:, 1, :], in0=duo[:, 1, :], in1=col_be1)
-
-            per_bank = BANK // P
+            nc.vector.tensor_mul(out=trio[:, 0, :], in0=col_g1, in1=rstd[:])
+            nc.vector.tensor_sub(out=trio[:, 1, :], in0=col_b1, in1=col_m1)
+            nc.vector.tensor_mul(out=trio[:, 1, :], in0=trio[:, 1, :], in1=trio[:, 0, :])
+            nc.vector.tensor_add(out=trio[:, 1, :], in0=trio[:, 1, :], in1=col_be1)
+            nc.vector.tensor_scalar_add(out=trio[:, 2, :], in0=col_bfc1, scalar1=1.0)
             ft_t = psum.tile([P, k_tiles, P], BF16, tag="bank")
             for kt in range(k_tiles):
                 nc.tensor.transpose(ft_t[:, kt, :], ft_sb[:, P * kt : P * (kt + 1)], ident_bf[:])
             nc.scalar.copy(out=ftT[:], in_=ft_t[:])
-            gate_acc = None
-            for step in range(rows + 1):
-                if step < rows:
-                    r = step
-                    wfc_t = psum.tile([P, k_tiles, P], BF16, tag="bank")
-                    for kt in range(k_tiles):
-                        nc.tensor.transpose(wfc_t[:, kt, :], wfc[:, r, P * kt : P * (kt + 1)], ident_bf[:])
-                    nc.scalar.copy(out=wfcT[:, :, P * r : P * (r + 1)], in_=wfc_t[:])
-                if step > 0:
-                    r = step - 1
-                    o_cols = slice(P * r, P * (r + 1))
-                    if r % per_bank == 0:
-                        gate_acc = psum.tile([P, per_bank, P], F32, tag="bank")
-                    for kt in range(k_tiles):
-                        nc.tensor.matmul(
-                            out=gate_acc[:, r % per_bank, :],
-                            lhsT=ftT[:, kt, :],
-                            rhs=wfcT[:, kt, o_cols],
-                            start=(kt == 0),
-                            stop=False,
-                        )
-                    nc.tensor.matmul(
-                        out=gate_acc[:, r % per_bank, :], lhsT=ones[:], rhs=bias_rows[:, o_cols], start=False, stop=True
-                    )
-                    if r % per_bank == per_bank - 1:
-                        nc.scalar.copy(
-                            out=gate[:, P * (r + 1 - per_bank) : P * (r + 1)],
-                            in_=gate_acc[:].rearrange("b q o -> b (q o)"),
-                        )
+            for r in range(rows):
+                wfc_t = psum.tile([P, k_tiles, P], BF16, tag="bank")
+                for kt in range(k_tiles):
+                    nc.tensor.transpose(wfc_t[:, kt, :], wfc[:, r, P * kt : P * (kt + 1)], ident_bf[:])
+                nc.scalar.copy(out=wfcT[:, :, P * r : P * (r + 1)], in_=wfc_t[:])
 
-            for v in range(2):
+            per_bank = N_TILE // P
+            for v in range(3):
                 for half in range(HALVES):
                     spread_t = psum.tile([P, per_bank, P], F32, tag="bank")
                     for q in range(per_bank):
                         r = per_bank * half + q
-                        nc.tensor.transpose(spread_t[:, q, :], duo[:, v, r : r + 1].to_broadcast([P, P]), ident_f32[:])
+                        nc.tensor.transpose(spread_t[:, q, :], trio[:, v, r : r + 1].to_broadcast([P, P]), ident_f32[:])
                     nc.vector.tensor_copy(
-                        out=spread[:, v, BANK * half : BANK * (half + 1)],
+                        out=spread[:, v, N_TILE * half : N_TILE * (half + 1)],
                         in_=spread_t[:].rearrange("b q o -> b (q o)"),
                     )
 
@@ -206,58 +175,51 @@ def tile_joint_module_pa_kernel(
                             in_=grouped[:, 0:n_pix].rearrange("p e b t -> p (e b t)"),
                         )
 
-        with ExitStack() as second_part:
-            second_part.enter_context(tc.manual_schedule())
-            plane_pool = second_part.enter_context(tc.tile_pool(name="planes", bufs=3))
-            store_pool = second_part.enter_context(tc.tile_pool(name="store", bufs=3))
-
-            def finish(o_tile, normed):
-                o_cols = slice(N_TILE * o_tile, N_TILE * (o_tile + 1))
-                result = store_pool.tile([P, N_TILE, PIX], F32)
-                nc.vector.scalar_tensor_tensor(
-                    out=result[:],
-                    in0=normed[:].rearrange("b x o -> b o x"),
-                    scalar=0.0,
-                    in1=gate[:, o_cols].unsqueeze(2).to_broadcast([P, N_TILE, PIX]),
-                    op0=ALU.max,
-                    op1=ALU.mult,
+        for half in range(HALVES):
+            o_cols = slice(N_TILE * half, N_TILE * (half + 1))
+            gate_acc = psum.tile([P, N_TILE], F32, tag="bank")
+            for kt in range(k_tiles):
+                nc.tensor.matmul(
+                    out=gate_acc[:],
+                    lhsT=ftT[:, kt, :],
+                    rhs=wfcT[:, kt, o_cols],
+                    start=(kt == 0),
+                    stop=(kt == k_tiles - 1),
                 )
-                nc.sync.dma_start(
-                    out=out_rows[:, PIX * N_TILE * o_tile : PIX * N_TILE * (o_tile + 1)],
-                    in_=result[:].rearrange("b o x -> b (o x)"),
-                )
+            nc.vector.tensor_add(out=gate[:, o_cols], in0=gate_acc[:], in1=spread[:, 2, o_cols])
 
-            previous = None
-            for o_tile in range(C_OUT // N_TILE):
-                o_cols = slice(N_TILE * o_tile, N_TILE * (o_tile + 1))
+        with tc.tile_pool(name="planes", bufs=2) as plane_pool, tc.tile_pool(name="store", bufs=4) as store_pool:
+            for half in range(HALVES):
+                o_cols = slice(N_TILE * half, N_TILE * (half + 1))
                 normed = plane_pool.tile([P, PIX, N_TILE], F32)
-                for first in range(0, PIX, PER_BANK):
-                    n_pix = min(PER_BANK, PIX - first)
-                    acc = psum.tile([P, PER_BANK, N_TILE], F32, tag="bank")
-                    for i in range(n_pix):
-                        b_cols = slice(P * (first + i), P * (first + i + 1))
-                        for g in range(PASSES):
-                            nc.tensor.matmul_mx(
-                                out=acc[:, i, :],
-                                lhsT=fv_codes[:, g, b_cols].bitcast(FP8X4),
-                                lhsT_scale=fv_scales[:, g, b_cols],
-                                rhs=w_words[:, g, 2 * N_TILE * o_tile : 2 * N_TILE * (o_tile + 1)].bitcast(FP4X4),
-                                rhs_scale=w_scales[:, g, o_cols],
-                                start=(g == 0),
-                                stop=(g == PASSES - 1),
-                            )
-                    block = normed[:, first : first + n_pix, :]
-                    nc.vector.tensor_mul(
-                        out=block,
-                        in0=acc[:, 0:n_pix, :],
-                        in1=spread[:, 0, o_cols].unsqueeze(1).to_broadcast([P, n_pix, N_TILE]),
+                for pix in range(PIX):
+                    b_cols = slice(P * pix, P * (pix + 1))
+                    acc = psum.tile([P, N_TILE], F32, tag="bank")
+                    for g in range(PASSES):
+                        nc.tensor.matmul_mx(
+                            out=acc[:],
+                            lhsT=fv_codes[:, g, b_cols].bitcast(FP8X4),
+                            lhsT_scale=fv_scales[:, g, b_cols],
+                            rhs=w_words[:, g, 2 * N_TILE * half : 2 * N_TILE * (half + 1)].bitcast(FP4X4),
+                            rhs_scale=w_scales[:, g, o_cols],
+                            start=(g == 0),
+                            stop=(g == PASSES - 1),
+                        )
+                    nc.vector.tensor_mul(out=normed[:, pix, :], in0=acc[:], in1=spread[:, 0, o_cols])
+                    nc.vector.tensor_add(out=normed[:, pix, :], in0=normed[:, pix, :], in1=spread[:, 1, o_cols])
+                for piece in range(N_TILE // O_STORE):
+                    o_lo = O_STORE * piece
+                    o_abs = N_TILE * half + o_lo
+                    result = store_pool.tile([P, O_STORE, PIX], F32)
+                    nc.vector.scalar_tensor_tensor(
+                        out=result[:],
+                        in0=normed[:, :, o_lo : o_lo + O_STORE].rearrange("b x o -> b o x"),
+                        scalar=0.0,
+                        in1=gate[:, o_abs : o_abs + O_STORE].unsqueeze(2).to_broadcast([P, O_STORE, PIX]),
+                        op0=ALU.max,
+                        op1=ALU.mult,
                     )
-                    shift = spread[:, 1, o_cols].unsqueeze(1).to_broadcast([P, n_pix, N_TILE])
-                    if n_pix == PER_BANK:
-                        nc.gpsimd.tensor_add(out=block, in0=block, in1=shift)
-                    else:
-                        nc.vector.tensor_add(out=block, in0=block, in1=shift)
-                    if first == 0 and previous is not None:
-                        finish(o_tile - 1, previous)
-                previous = normed
-            finish(C_OUT // N_TILE - 1, previous)
+                    nc.sync.dma_start(
+                        out=out_rows[:, PIX * o_abs : PIX * (o_abs + O_STORE)],
+                        in_=result[:].rearrange("b o x -> b (o x)"),
+                    )

@@ -25,7 +25,6 @@ PASSES = C_IN // K_PASS
 N_TILE = 512
 HALVES = C_OUT // N_TILE
 PAIRS = (PIX + 1) // 2
-ODD_PITCH = 2 * PAIRS
 O_STORE = 128
 
 FLOPS = 2 * P * PIX * C_IN * C_OUT + 2 * P * C_TXT * C_OUT
@@ -135,44 +134,34 @@ def tile_joint_module_pa_kernel(
                         in_=spread_t[:].rearrange("b q o -> b (q o)"),
                     )
 
-            odd_bufs = 3
-            odd_tiles = [front.tile([P, (K_PASS // 2) * ODD_PITCH], BF16, name="odd%d" % i) for i in range(odd_bufs)]
-            for odd in odd_tiles:
-                nc.vector.memset(odd[:], 0.0)
-            with tc.tile_pool(name="regroup", bufs=4) as regroup:
+            with tc.tile_pool(name="regroup", bufs=4) as regroup, tc.tile_pool(name="spaced", bufs=2) as spaced_pool:
                 for g in range(PASSES):
-                    odd = odd_tiles[g % odd_bufs]
-                    nc.vector.tensor_copy(
-                        out=odd[:].rearrange("b (c x) -> b c x", x=ODD_PITCH)[:, :, 0:PIX],
-                        in_=fv_sb[:, g, :].rearrange("b (c two x) -> b c two x", two=2, x=PIX)[:, :, 1, :],
-                    )
-                    even_words = fv_sb[:, g, :].bitcast(F32).rearrange("b (p w) -> b p w", p=P)
-                    odd_words = odd[:].bitcast(F32).rearrange("b (p w) -> b p w", p=P)
+                    spaced = spaced_pool.tile([P, PIX, 2, P, 2], BF16)
+                    by_channel = fv_sb[:, g, :].rearrange("b (p u e x) -> b p u e x", u=2, e=2, x=PIX)
+                    for x0 in range(0, PIX, 3):
+                        for u in range(2):
+                            nc.vector.tensor_copy(
+                                out=spaced[:, x0 : x0 + 3, u].rearrange("b x p e -> b p e x"),
+                                in_=by_channel[:, :, u, :, x0 : x0 + 3],
+                            )
+                    spaced_words = spaced[:].rearrange("b x u p e -> b (x u p e)").bitcast(F32)
                     for pair in range(PAIRS):
                         n_pix = min(2, PIX - 2 * pair)
-                        planes = psum.tile([P, PACK, P], F32, tag="bank")
-                        for t in range(PACK):
-                            if t % 2 == 0:
-                                words = even_words[:, :, PIX * (t // 2) + pair]
-                            else:
-                                words = odd_words[:, :, PAIRS * (t // 2) + pair]
-                            nc.tensor.transpose(planes[:, t, :], words, ident_f32[:])
-                        grouped = regroup.tile([P, 2, P, PACK], BF16, align_bytes=64)
-                        by_pixel = (
-                            planes[:]
-                            .rearrange("p t b -> p (t b)")
-                            .bitcast(BF16)
-                            .rearrange("p (t b e) -> p e b t", t=PACK, e=2)
+                        planes = psum.tile([P, 2, 2, P], F32, tag="bank")
+                        for e in range(n_pix):
+                            for u in range(2):
+                                word0 = P * (2 * (2 * pair + e) + u)
+                                nc.tensor.transpose(planes[:, e, u, :], spaced_words[:, word0 : word0 + P], ident_f32[:])
+                        grouped = regroup.tile([P, 2 * P * PACK], BF16, align_bytes=64)
+                        nc.scalar.copy(
+                            out=grouped[:, 0 : n_pix * P * PACK].bitcast(F32).rearrange("p (e b u) -> p e b u", b=P, u=2),
+                            in_=planes[:, 0:n_pix].rearrange("p e u b -> p e b u"),
                         )
-                        if pair < PAIRS - 2 or (pair == PAIRS - 2 and g % 2 == 0):
-                            nc.scalar.copy(out=grouped[:], in_=by_pixel)
-                        else:
-                            nc.vector.tensor_copy(out=grouped[:, 0:n_pix], in_=by_pixel[:, 0:n_pix])
                         cols_q = slice(2 * P * pair, 2 * P * pair + P * n_pix)
                         nc.vector.quantize_mx(
                             out=fv_codes[:, g, cols_q].bitcast(FP8X4),
                             scales=fv_scales[:, g, cols_q],
-                            in_=grouped[:, 0:n_pix].rearrange("p e b t -> p (e b t)"),
+                            in_=grouped[:, 0 : n_pix * P * PACK],
                         )
 
         for half in range(HALVES):

@@ -10,7 +10,6 @@ U32 = mybir.dt.uint32
 U8 = mybir.dt.uint8
 FP8X4 = mybir.dt.float8_e4m3fn_x4
 FP4X4 = mybir.dt.float4_e2m1fn_x4
-ALU = mybir.AluOpType
 ACT = mybir.ActivationFunctionType
 
 P = 128
@@ -22,10 +21,15 @@ EPS = 1e-5
 PACK = 4
 K_PASS = P * PACK
 PASSES = C_IN // K_PASS
-N_TILE = 512
-HALVES = C_OUT // N_TILE
 PAIRS = (PIX + 1) // 2
-O_STORE = 128
+BANK = 512
+COLS = PIX * P
+O_TILES = C_OUT // P
+SQ = 32
+BLKS = P // SQ
+FIRST_PARTS = 2
+PER_BANK = BANK // P
+TRI = 3
 
 FLOPS = 2 * P * PIX * C_IN * C_OUT + 2 * P * C_TXT * C_OUT
 
@@ -41,174 +45,260 @@ def tile_joint_module_pa_kernel(
     with ExitStack() as ctx:
         keep = ctx.enter_context(tc.tile_pool(name="keep", bufs=1))
         psum = ctx.enter_context(tc.psum_pool(name="psum", bufs=8))
+        spaced_pool = ctx.enter_context(tc.tile_pool(name="spaced", bufs=2))
+        regroup = ctx.enter_context(tc.tile_pool(name="regroup", bufs=4))
+        work = ctx.enter_context(tc.tile_pool(name="work", bufs=2))
+        store_pool = ctx.enter_context(tc.tile_pool(name="store", bufs=3))
 
         vectors = [b1, g1, be1, m1, v1, bfc1]
         rows = C_OUT // P
         k_tiles = C_TXT // P
 
-        w_words = keep.tile([P, PASSES, 2 * C_OUT], U8, align_bytes=64)
-        fv_codes = keep.tile([P, PASSES, PIX * P], U32, align_bytes=64)
-        fv_scales = keep.tile([P, PASSES, PIX * P], U8, align_bytes=64)
+        w_words = [keep.tile([P, 2 * C_OUT], U8, align_bytes=64, name="w_words%d" % g) for g in range(PASSES)]
+        w_scales = keep.tile([P, PASSES, C_OUT], U8, align_bytes=64)
+        fv_codes = [keep.tile([P, COLS], U32, align_bytes=64, name="fv_codes%d" % g) for g in range(PASSES)]
+        fv_scales = [keep.tile([P, COLS], U8, align_bytes=64, name="fv_scales%d" % g) for g in range(PASSES)]
+        fv_sb = [keep.tile([P, chunk], BF16, name="fv_sb%d" % g) for g in range(PASSES)]
+        ft_sb = keep.tile([P, C_TXT], BF16)
+        wfc = [keep.tile([P, C_TXT], BF16, name="wfc%d" % r) for r in range(rows)]
         cols = keep.tile([P, len(vectors), rows], F32)
         std = keep.tile([P, rows], F32)
         rstd = keep.tile([P, rows], F32)
-        trio = keep.tile([P, 3, rows], F32)
-        spread = keep.tile([P, 3, C_OUT], F32)
+        scale = keep.tile([P, rows], F32)
+        shift = keep.tile([P, rows], F32)
+        gate_bias = keep.tile([P, rows], F32)
         ftT = keep.tile([P, k_tiles, P], BF16)
         wfcT = keep.tile([P, k_tiles, C_OUT], BF16)
-        gate = keep.tile([P, C_OUT], F32)
+        gate_o = keep.tile([P, O_TILES * P], F32, align_bytes=64)
+        gate_t = keep.tile([P, O_TILES * P], F32, align_bytes=64)
 
-        ident_bf = keep.tile([P, P], BF16)
-        make_identity(nc, ident_bf[:])
         ident_f32 = keep.tile([P, P], F32)
         make_identity(nc, ident_f32[:])
+        ident_bf = keep.tile([P, P], BF16)
+        make_identity(nc, ident_bf[:])
+        nc.gpsimd.memset(w_scales[:].rearrange("p g n -> p (g n)").bitcast(I32), 0)
+        vec_rows = keep.tile([P, P], BF16)
+        nc.vector.memset(vec_rows[:], 0.0)
 
         warm = keep.tile([P, 1], F32)
         nc.vector.memset(warm[:], 1.0)
         nc.scalar.activation(out=warm[:], in_=warm[:], func=ACT.Sqrt)
 
-        vec_rows = keep.tile([P, P], BF16)
-        nc.vector.memset(vec_rows[:], 0.0)
-        w_scales = keep.tile([P, PASSES, C_OUT], U8, align_bytes=64)
-        nc.vector.memset(w_scales[:].rearrange("p g n -> p (g n)").bitcast(I32), 0)
+        def load_fv(g, parts=1):
+            step = chunk // parts
+            for lo in range(0, chunk, step):
+                nc.sync.dma_start(
+                    out=fv_sb[g][:, lo : lo + step], in_=fv_rows[:, chunk * g + lo : chunk * g + lo + step]
+                )
 
+        def load_words(g):
+            nc.sync.dma_start(out=w_words[g][:].bitcast(I32), in_=W1_words[g].bitcast(I32))
+
+        load_fv(0, FIRST_PARTS)
+        load_fv(1)
+        for quad in range(4):
+            nc.sync.dma_start(
+                out=w_scales[32 * quad : 32 * quad + 4].bitcast(I32),
+                in_=W1_scales[:, 4 * quad : 4 * quad + 4, :].rearrange("g r n -> r g n").bitcast(I32),
+            )
+        for g in range(3):
+            load_words(g)
+        load_fv(2)
+        load_fv(3)
+        for g in range(3, PASSES):
+            load_words(g)
         for v, vector in enumerate(vectors):
             nc.sync.dma_start(
                 out=vec_rows[rows * v : rows * (v + 1), :],
                 in_=vector.rearrange("(r c) -> r c", c=P),
             )
+        nc.sync.dma_start(out=ft_sb[:], in_=ft)
+        load_fv(4)
+        for r in range(rows // 2):
+            nc.sync.dma_start(out=wfc[r][:], in_=Wfc1[P * r : P * (r + 1), :])
+        load_fv(5)
+        for r in range(rows // 2, rows):
+            nc.sync.dma_start(out=wfc[r][:], in_=Wfc1[P * r : P * (r + 1), :])
 
-        with tc.tile_pool(name="front", bufs=1) as front:
-            ft_sb = front.tile([P, C_TXT], BF16)
-            nc.sync.dma_start(out=ft_sb[:], in_=ft)
-            wfc = front.tile([P, rows, C_TXT], BF16)
-            wfc_dram = Wfc1.rearrange("(r p) k -> p r k", p=P)
-            for r in range(rows):
-                nc.sync.dma_start(out=wfc[:, r, :], in_=wfc_dram[:, r, :])
-            fv_sb = front.tile([P, PASSES, chunk], BF16)
-            for g in range(PASSES):
-                nc.sync.dma_start(out=fv_sb[:, g, :], in_=fv_rows[:, chunk * g : chunk * (g + 1)])
-            nc.sync.dma_start(
-                out=w_words[:].bitcast(I32),
-                in_=W1_words.rearrange("g p n -> p g n").bitcast(I32),
-            )
-            for quad in range(4):
-                nc.sync.dma_start(
-                    out=w_scales[32 * quad : 32 * quad + 4].bitcast(I32),
-                    in_=W1_scales[:, 4 * quad : 4 * quad + 4, :].rearrange("g r n -> r g n").bitcast(I32),
+        def sort_by_pixel(g):
+            spaced = spaced_pool.tile([P, PIX, 2, P, 2], BF16)
+            by_channel = fv_sb[g][:].rearrange("b (p u e x) -> b p u e x", u=2, e=2, x=PIX)
+            parts = FIRST_PARTS if g == 0 else 1
+            for part in range(parts):
+                p_s = slice(P // parts * part, P // parts * (part + 1))
+                for x0 in range(0, PIX, TRI):
+                    for u in range(2):
+                        nc.vector.tensor_copy(
+                            out=spaced[:, x0 : x0 + TRI, u, p_s, :].rearrange("b x p e -> b p e x"),
+                            in_=by_channel[:, p_s, u, :, x0 : x0 + TRI],
+                        )
+            return spaced
+
+        def quantise(g, spaced):
+            spaced_words = spaced[:].rearrange("b x u p e -> b (x u p e)").bitcast(F32)
+            for pair in range(PAIRS):
+                n_pix = min(2, PIX - 2 * pair)
+                planes = psum.tile([P, 2, 2, P], F32, tag="bank")
+                for e in range(n_pix):
+                    for u in range(2):
+                        word0 = P * (2 * (2 * pair + e) + u)
+                        nc.tensor.transpose(planes[:, e, u, :], spaced_words[:, word0 : word0 + P], ident_f32[:])
+                grouped = regroup.tile([P, 2 * P * PACK], BF16, align_bytes=64)
+                nc.scalar.copy(
+                    out=grouped[:, 0 : n_pix * P * PACK].bitcast(F32).rearrange("p (e b u) -> p e b u", b=P, u=2),
+                    in_=planes[:, 0:n_pix].rearrange("p e u b -> p e b u"),
+                )
+                cols_q = slice(2 * P * pair, 2 * P * pair + P * n_pix)
+                nc.vector.quantize_mx(
+                    out=fv_codes[g][:, cols_q].bitcast(FP8X4),
+                    scales=fv_scales[g][:, cols_q],
+                    in_=grouped[:, 0 : n_pix * P * PACK],
                 )
 
-            vec_t = psum.tile([P, P], BF16, tag="bank")
-            nc.tensor.transpose(vec_t[:], vec_rows[:], ident_bf[:])
-            nc.vector.tensor_copy(
-                out=cols[:], in_=vec_t[:, 0 : len(vectors) * rows].rearrange("p (v r) -> p v r", r=rows)
-            )
-            col_b1, col_g1, col_be1, col_m1, col_v1, col_bfc1 = [cols[:, v, :] for v in range(len(vectors))]
-            nc.vector.tensor_scalar_add(out=std[:], in0=col_v1, scalar1=EPS)
-            nc.scalar.activation(out=std[:], in_=std[:], func=ACT.Sqrt)
-            nc.vector.reciprocal(out=rstd[:], in_=std[:])
-            nc.vector.tensor_mul(out=trio[:, 0, :], in0=col_g1, in1=rstd[:])
-            nc.vector.tensor_sub(out=trio[:, 1, :], in0=col_b1, in1=col_m1)
-            nc.vector.tensor_mul(out=trio[:, 1, :], in0=trio[:, 1, :], in1=trio[:, 0, :])
-            nc.vector.tensor_add(out=trio[:, 1, :], in0=trio[:, 1, :], in1=col_be1)
-            nc.vector.tensor_scalar_add(out=trio[:, 2, :], in0=col_bfc1, scalar1=1.0)
-            ft_t = psum.tile([P, k_tiles, P], BF16, tag="bank")
-            for kt in range(k_tiles):
-                nc.tensor.transpose(ft_t[:, kt, :], ft_sb[:, P * kt : P * (kt + 1)], ident_bf[:])
-            nc.scalar.copy(out=ftT[:], in_=ft_t[:])
-            for r in range(rows):
-                wfc_t = psum.tile([P, k_tiles, P], BF16, tag="bank")
-                for kt in range(k_tiles):
-                    nc.tensor.transpose(wfc_t[:, kt, :], wfc[:, r, P * kt : P * (kt + 1)], ident_bf[:])
-                nc.scalar.copy(out=wfcT[:, :, P * r : P * (r + 1)], in_=wfc_t[:])
+        col_slices = [slice(c, min(c + BANK, COLS)) for c in range(0, COLS, BANK)]
 
-            per_bank = N_TILE // P
-            for v in range(3):
-                for half in range(HALVES):
-                    spread_t = psum.tile([P, per_bank, P], F32, tag="bank")
-                    for q in range(per_bank):
-                        r = per_bank * half + q
-                        nc.tensor.transpose(spread_t[:, q, :], trio[:, v, r : r + 1].to_broadcast([P, P]), ident_f32[:])
-                    nc.vector.tensor_copy(
-                        out=spread[:, v, N_TILE * half : N_TILE * (half + 1)],
-                        in_=spread_t[:].rearrange("b q o -> b (q o)"),
-                    )
-
-            with tc.tile_pool(name="regroup", bufs=4) as regroup, tc.tile_pool(name="spaced", bufs=2) as spaced_pool:
-                for g in range(PASSES):
-                    spaced = spaced_pool.tile([P, PIX, 2, P, 2], BF16)
-                    by_channel = fv_sb[:, g, :].rearrange("b (p u e x) -> b p u e x", u=2, e=2, x=PIX)
-                    for x0 in range(0, PIX, 3):
-                        for u in range(2):
-                            nc.vector.tensor_copy(
-                                out=spaced[:, x0 : x0 + 3, u].rearrange("b x p e -> b p e x"),
-                                in_=by_channel[:, :, u, :, x0 : x0 + 3],
-                            )
-                    spaced_words = spaced[:].rearrange("b x u p e -> b (x u p e)").bitcast(F32)
-                    for pair in range(PAIRS):
-                        n_pix = min(2, PIX - 2 * pair)
-                        planes = psum.tile([P, 2, 2, P], F32, tag="bank")
-                        for e in range(n_pix):
-                            for u in range(2):
-                                word0 = P * (2 * (2 * pair + e) + u)
-                                nc.tensor.transpose(planes[:, e, u, :], spaced_words[:, word0 : word0 + P], ident_f32[:])
-                        grouped = regroup.tile([P, 2 * P * PACK], BF16, align_bytes=64)
-                        nc.scalar.copy(
-                            out=grouped[:, 0 : n_pix * P * PACK].bitcast(F32).rearrange("p (e b u) -> p e b u", b=P, u=2),
-                            in_=planes[:, 0:n_pix].rearrange("p e u b -> p e b u"),
-                        )
-                        cols_q = slice(2 * P * pair, 2 * P * pair + P * n_pix)
-                        nc.vector.quantize_mx(
-                            out=fv_codes[:, g, cols_q].bitcast(FP8X4),
-                            scales=fv_scales[:, g, cols_q],
-                            in_=grouped[:, 0 : n_pix * P * PACK],
-                        )
-
-        for half in range(HALVES):
-            o_cols = slice(N_TILE * half, N_TILE * (half + 1))
-            gate_acc = psum.tile([P, N_TILE], F32, tag="bank")
-            for kt in range(k_tiles):
-                nc.tensor.matmul(
-                    out=gate_acc[:],
-                    lhsT=ftT[:, kt, :],
-                    rhs=wfcT[:, kt, o_cols],
-                    start=(kt == 0),
-                    stop=(kt == k_tiles - 1),
+        def multiply(t, accs, g, banks):
+            for k in banks:
+                width = col_slices[k].stop - col_slices[k].start
+                nc.tensor.matmul_mx(
+                    out=accs[k][:, 0:width],
+                    lhsT=w_words[g][:, 2 * P * t : 2 * P * (t + 1)].bitcast(FP4X4),
+                    lhsT_scale=w_scales[:, g, P * t : P * (t + 1)],
+                    rhs=fv_codes[g][:, col_slices[k]].bitcast(FP8X4),
+                    rhs_scale=fv_scales[g][:, col_slices[k]],
+                    start=(g == 0),
+                    stop=(g == PASSES - 1),
                 )
-            nc.vector.tensor_add(out=gate[:, o_cols], in0=gate_acc[:], in1=spread[:, 2, o_cols])
 
-        with tc.tile_pool(name="planes", bufs=2) as plane_pool, tc.tile_pool(name="store", bufs=4) as store_pool:
-            for half in range(HALVES):
-                o_cols = slice(N_TILE * half, N_TILE * (half + 1))
-                normed = plane_pool.tile([P, PIX, N_TILE], F32)
-                for pix in range(PIX):
-                    b_cols = slice(P * pix, P * (pix + 1))
-                    acc = psum.tile([P, N_TILE], F32, tag="bank")
-                    for g in range(PASSES):
-                        nc.tensor.matmul_mx(
-                            out=acc[:],
-                            lhsT=fv_codes[:, g, b_cols].bitcast(FP8X4),
-                            lhsT_scale=fv_scales[:, g, b_cols],
-                            rhs=w_words[:, g, 2 * N_TILE * half : 2 * N_TILE * (half + 1)].bitcast(FP4X4),
-                            rhs_scale=w_scales[:, g, o_cols],
-                            start=(g == 0),
-                            stop=(g == PASSES - 1),
-                        )
-                    nc.vector.tensor_mul(out=normed[:, pix, :], in0=acc[:], in1=spread[:, 0, o_cols])
-                    nc.vector.tensor_add(out=normed[:, pix, :], in0=normed[:, pix, :], in1=spread[:, 1, o_cols])
-                for piece in range(N_TILE // O_STORE):
-                    o_lo = O_STORE * piece
-                    o_abs = N_TILE * half + o_lo
-                    result = store_pool.tile([P, O_STORE, PIX], F32)
-                    nc.vector.scalar_tensor_tensor(
-                        out=result[:],
-                        in0=normed[:, :, o_lo : o_lo + O_STORE].rearrange("b x o -> b o x"),
-                        scalar=0.0,
-                        in1=gate[:, o_abs : o_abs + O_STORE].unsqueeze(2).to_broadcast([P, O_STORE, PIX]),
-                        op0=ALU.max,
-                        op1=ALU.mult,
-                    )
+        def new_accs():
+            accs = []
+            for k in range(len(col_slices)):
+                acc = psum.tile([P, BANK], F32, tag="bank", name="acc")
+                accs.append(acc)
+            return accs
+
+        def transpose_wfc(r):
+            wfc_t = psum.tile([P, k_tiles, P], BF16, tag="bank")
+            for kt in range(k_tiles):
+                nc.tensor.transpose(wfc_t[:, kt, :], wfc[r][:, P * kt : P * (kt + 1)], ident_bf[:])
+            nc.scalar.copy(out=wfcT[:, :, P * r : P * (r + 1)], in_=wfc_t[:])
+
+        def epilogue(t, accs):
+            normed = work.tile([P, COLS], F32, align_bytes=64)
+            for k, cs in enumerate(col_slices):
+                nc.scalar.activation(
+                    out=normed[:, cs],
+                    in_=accs[k][:, 0 : cs.stop - cs.start],
+                    func=ACT.Relu,
+                    scale=scale[:, t : t + 1],
+                    bias=shift[:, t : t + 1],
+                )
+            turned = work.tile([P, COLS], F32, align_bytes=64)
+            for cs in col_slices:
+                nc.vector.transpose(out=turned[:, cs], in_=normed[:, cs])
+            last = t == O_TILES - 1
+            by_three = work.tile([P, TRI, P, TRI], F32)
+            turned_g = turned[:].rearrange("p (g x n) -> p g n x", g=TRI, x=TRI)
+            if last:
+                for grp in range(TRI):
+                    nc.scalar.copy(out=by_three[:, grp], in_=turned_g[:, grp])
+            else:
+                nc.scalar.copy(out=by_three[:], in_=turned_g)
+            result = store_pool.tile([P, P, PIX], F32)
+            parts = 2 if last else 1
+            blks = BLKS // parts
+            for part in range(parts):
+                n_s = slice(P // parts * part, P // parts * (part + 1))
+                gate = gate_t[:, P * t + n_s.start : P * t + n_s.stop]
+                nc.vector.tensor_mul(
+                    out=result[:, n_s].rearrange("p n (g x) -> p n g x", g=TRI),
+                    in0=by_three[:, :, n_s].rearrange("p g n x -> p n g x"),
+                    in1=gate.unsqueeze(2).unsqueeze(3).to_broadcast([P, P // parts, TRI, TRI]),
+                )
+                for i in range(BLKS):
+                    o_lo = P * t + SQ * i
+                    by_block = out_rows[SQ * blks * part : SQ * blks * (part + 1), PIX * o_lo : PIX * (o_lo + SQ)]
                     nc.sync.dma_start(
-                        out=out_rows[:, PIX * o_abs : PIX * (o_abs + O_STORE)],
-                        in_=result[:].rearrange("b o x -> b (o x)"),
+                        out=by_block.rearrange("(j c) n -> c j n", c=SQ),
+                        in_=result[SQ * i : SQ * (i + 1), n_s].rearrange("c (j r) x -> c j (r x)", j=blks),
                     )
+
+        def text_gate(half):
+            gate_acc = psum.tile([P, PER_BANK, P], F32, tag="bank")
+            for q in range(PER_BANK):
+                t = PER_BANK * half + q
+                for kt in range(k_tiles):
+                    nc.tensor.matmul(
+                        out=gate_acc[:, q, :],
+                        lhsT=wfcT[:, kt, P * t : P * (t + 1)],
+                        rhs=ftT[:, kt, :],
+                        start=(kt == 0),
+                        stop=(kt == k_tiles - 1),
+                    )
+            h_cols = slice(BANK * half, BANK * (half + 1))
+            nc.vector.tensor_add(
+                out=gate_o[:, h_cols].rearrange("p (q b) -> p q b", b=P),
+                in0=gate_acc[:],
+                in1=gate_bias[:, PER_BANK * half : PER_BANK * (half + 1)].unsqueeze(2).to_broadcast([P, PER_BANK, P]),
+            )
+            nc.vector.transpose(out=gate_t[:, h_cols], in_=gate_o[:, h_cols])
+
+        all_banks = list(range(len(col_slices)))
+        early_banks = all_banks[0:2]
+        accs0 = new_accs()
+        accs1 = []
+        for k in early_banks:
+            acc = psum.tile([P, BANK], F32, tag="bank", name="acc")
+            accs1.append(acc)
+
+        def early_passes(g):
+            multiply(0, accs0, g, all_banks)
+            multiply(1, accs1, g, early_banks)
+
+        for g in range(PASSES):
+            spaced = sort_by_pixel(g)
+            quantise(g, spaced)
+            if g > 0:
+                early_passes(g - 1)
+            if g == 3:
+                vec_t = psum.tile([P, P], BF16, tag="bank")
+                nc.tensor.transpose(vec_t[:], vec_rows[:], ident_bf[:])
+                nc.vector.tensor_copy(
+                    out=cols[:], in_=vec_t[:, 0 : len(vectors) * rows].rearrange("p (v r) -> p v r", r=rows)
+                )
+                col_b1, col_g1, col_be1, col_m1, col_v1, col_bfc1 = [cols[:, v, :] for v in range(len(vectors))]
+                nc.vector.tensor_scalar_add(out=std[:], in0=col_v1, scalar1=EPS)
+                nc.scalar.activation(out=std[:], in_=std[:], func=ACT.Sqrt)
+                nc.vector.reciprocal(out=rstd[:], in_=std[:])
+                nc.vector.tensor_mul(out=scale[:], in0=col_g1, in1=rstd[:])
+                nc.vector.tensor_sub(out=shift[:], in0=col_b1, in1=col_m1)
+                nc.vector.tensor_mul(out=shift[:], in0=shift[:], in1=scale[:])
+                nc.vector.tensor_add(out=shift[:], in0=shift[:], in1=col_be1)
+                nc.vector.tensor_scalar_add(out=gate_bias[:], in0=col_bfc1, scalar1=1.0)
+                ft_t = psum.tile([P, k_tiles, P], BF16, tag="bank")
+                for kt in range(k_tiles):
+                    nc.tensor.transpose(ft_t[:, kt, :], ft_sb[:, P * kt : P * (kt + 1)], ident_bf[:])
+                nc.scalar.copy(out=ftT[:], in_=ft_t[:])
+            if g == 4:
+                for r in range(rows // 2):
+                    transpose_wfc(r)
+        text_gate(0)
+        early_passes(PASSES - 1)
+        epilogue(0, accs0)
+
+        for t in range(1, O_TILES):
+            if t == 1:
+                acc = psum.tile([P, BANK], F32, tag="bank", name="acc")
+                accs = accs1 + [acc]
+                todo = all_banks[2:]
+            else:
+                accs = new_accs()
+                todo = all_banks
+            for k in todo:
+                for g in range(PASSES):
+                    multiply(t, accs, g, [k])
+            epilogue(t, accs)
+            if t == 1:
+                for r in range(rows // 2, rows):
+                    transpose_wfc(r)
+                text_gate(1)

@@ -96,6 +96,7 @@ def tile_joint_module_pa_kernel(
 
         load_fv(0, FIRST_PARTS)
         load_fv(1)
+        load_fv(2)
         for quad in range(4):
             nc.sync.dma_start(
                 out=w_scales[32 * quad : 32 * quad + 4].bitcast(I32),
@@ -103,17 +104,16 @@ def tile_joint_module_pa_kernel(
             )
         for g in range(3):
             load_words(g)
-        load_fv(2)
         load_fv(3)
         for g in range(3, PASSES):
             load_words(g)
+        load_fv(4)
         for v, vector in enumerate(vectors):
             nc.sync.dma_start(
                 out=vec_rows[rows * v : rows * (v + 1), :],
                 in_=vector.rearrange("(r c) -> r c", c=P),
             )
         nc.sync.dma_start(out=ft_sb[:], in_=ft)
-        load_fv(4)
         for r in range(rows // 2):
             nc.sync.dma_start(out=wfc[r][:], in_=Wfc1[P * r : P * (r + 1), :])
         load_fv(5)
@@ -126,12 +126,16 @@ def tile_joint_module_pa_kernel(
             parts = FIRST_PARTS if g == 0 else 1
             for part in range(parts):
                 p_s = slice(P // parts * part, P // parts * (part + 1))
-                for x0 in range(0, PIX, TRI):
+                for x0 in range(0, PIX - 1, 4):
                     for u in range(2):
                         nc.vector.tensor_copy(
-                            out=spaced[:, x0 : x0 + TRI, u, p_s, :].rearrange("b x p e -> b p e x"),
-                            in_=by_channel[:, p_s, u, :, x0 : x0 + TRI],
+                            out=spaced[:, x0 : x0 + 4, u, p_s, :].rearrange("b (h x) p e -> b h p e x", h=2),
+                            in_=by_channel[:, p_s, u, :, x0 : x0 + 4].rearrange("b p e (h x) -> b h p e x", h=2),
                         )
+                nc.vector.tensor_copy(
+                    out=spaced[:, PIX - 1, :, p_s, :].rearrange("b u p e -> b p u e"),
+                    in_=by_channel[:, p_s, :, :, PIX - 1],
+                )
             return spaced
 
         def quantise(g, spaced):
@@ -258,7 +262,9 @@ def tile_joint_module_pa_kernel(
         for g in range(PASSES):
             spaced = sort_by_pixel(g)
             quantise(g, spaced)
-            if g > 0:
+            if g == 2:
+                early_passes(0)
+            if g >= 2:
                 early_passes(g - 1)
             if g == 3:
                 vec_t = psum.tile([P, P], BF16, tag="bank")

@@ -29,6 +29,8 @@ SQ = 32
 BLKS = P // SQ
 FIRST_PARTS = 2
 PER_BANK = BANK // P
+WARM_START = 6
+WARM_PAIRS = ((0, 1, 2, 3, 4), (0, 2, 4), (), (), (), ())
 TRI = 3
 
 FLOPS = 2 * P * PIX * C_IN * C_OUT + 2 * P * C_TXT * C_OUT
@@ -45,8 +47,8 @@ def tile_joint_module_pa_kernel(
     with ExitStack() as ctx:
         keep = ctx.enter_context(tc.tile_pool(name="keep", bufs=1))
         psum = ctx.enter_context(tc.psum_pool(name="psum", bufs=8))
-        spaced_pool = ctx.enter_context(tc.tile_pool(name="spaced", bufs=2))
-        regroup = ctx.enter_context(tc.tile_pool(name="regroup", bufs=4))
+        spaced_pool = ctx.enter_context(tc.tile_pool(name="spaced", bufs=3))
+        regroup = ctx.enter_context(tc.tile_pool(name="regroup", bufs=6))
         work = ctx.enter_context(tc.tile_pool(name="work", bufs=2))
         store_pool = ctx.enter_context(tc.tile_pool(name="store", bufs=3))
 
@@ -79,6 +81,8 @@ def tile_joint_module_pa_kernel(
         nc.gpsimd.memset(w_scales[:].rearrange("p g n -> p (g n)").bitcast(I32), 0)
         vec_rows = keep.tile([P, P], BF16)
         nc.vector.memset(vec_rows[:], 0.0)
+        zeros = keep.tile([P, BANK], BF16)
+        nc.vector.memset(zeros[:], 0.0)
 
         warm = keep.tile([P, 1], F32)
         nc.vector.memset(warm[:], 1.0)
@@ -94,9 +98,21 @@ def tile_joint_module_pa_kernel(
         def load_words(g):
             nc.sync.dma_start(out=w_words[g][:].bitcast(I32), in_=W1_words[g].bitcast(I32))
 
+        def load_wfc(r_lo, r_hi):
+            for r in range(r_lo, r_hi):
+                nc.sync.dma_start(out=wfc[r][:], in_=Wfc1[P * r : P * (r + 1), :])
+
         load_fv(0, FIRST_PARTS)
+        for v, vector in enumerate(vectors):
+            nc.sync.dma_start(
+                out=vec_rows[rows * v : rows * (v + 1), :],
+                in_=vector.rearrange("(r c) -> r c", c=P),
+            )
         load_fv(1)
         load_fv(2)
+        nc.sync.dma_start(out=ft_sb[:], in_=ft)
+        load_wfc(0, rows // 2)
+        load_fv(3)
         for quad in range(4):
             nc.sync.dma_start(
                 out=w_scales[32 * quad : 32 * quad + 4].bitcast(I32),
@@ -104,112 +120,228 @@ def tile_joint_module_pa_kernel(
             )
         for g in range(3):
             load_words(g)
-        load_fv(3)
+        load_fv(4)
+        load_wfc(rows // 2, rows)
+        load_fv(5)
         for g in range(3, PASSES):
             load_words(g)
-        load_fv(4)
-        for v, vector in enumerate(vectors):
-            nc.sync.dma_start(
-                out=vec_rows[rows * v : rows * (v + 1), :],
-                in_=vector.rearrange("(r c) -> r c", c=P),
-            )
-        nc.sync.dma_start(out=ft_sb[:], in_=ft)
-        for r in range(rows // 2):
-            nc.sync.dma_start(out=wfc[r][:], in_=Wfc1[P * r : P * (r + 1), :])
-        load_fv(5)
-        for r in range(rows // 2, rows):
-            nc.sync.dma_start(out=wfc[r][:], in_=Wfc1[P * r : P * (r + 1), :])
 
-        def sort_by_pixel(g):
-            spaced = spaced_pool.tile([P, PIX, 2, P, 2], BF16)
+        ctx.enter_context(
+            tc.manual_schedule(
+                engines={mybir.EngineType.PE, mybir.EngineType.DVE, mybir.EngineType.Activation}
+            )
+        )
+
+        def sort_parts(g, spaced):
             by_channel = fv_sb[g][:].rearrange("b (p u e x) -> b p u e x", u=2, e=2, x=PIX)
+
+            def four(x0, u, p_s):
+                return lambda: nc.vector.tensor_copy(
+                    out=spaced[:, x0 : x0 + 4, u, p_s, :].rearrange("b (h x) p e -> b h p e x", h=2),
+                    in_=by_channel[:, p_s, u, :, x0 : x0 + 4].rearrange("b p e (h x) -> b h p e x", h=2),
+                )
+
+            def last_pixel(copy):
+                return lambda: copy(
+                    out=spaced[:, PIX - 1].rearrange("b u p e -> b p u e"), in_=by_channel[:, :, :, :, PIX - 1]
+                )
+
             parts = FIRST_PARTS if g == 0 else 1
+            calls = []
             for part in range(parts):
                 p_s = slice(P // parts * part, P // parts * (part + 1))
                 for x0 in range(0, PIX - 1, 4):
                     for u in range(2):
-                        nc.vector.tensor_copy(
-                            out=spaced[:, x0 : x0 + 4, u, p_s, :].rearrange("b (h x) p e -> b h p e x", h=2),
-                            in_=by_channel[:, p_s, u, :, x0 : x0 + 4].rearrange("b p e (h x) -> b h p e x", h=2),
-                        )
-                nc.vector.tensor_copy(
-                    out=spaced[:, PIX - 1, :, p_s, :].rearrange("b u p e -> b p u e"),
-                    in_=by_channel[:, p_s, :, :, PIX - 1],
-                )
-            return spaced
+                        calls.append(four(x0, u, p_s))
+            return calls, last_pixel(nc.scalar.copy)
 
-        def quantise(g, spaced):
+        def new_spaced():
+            return spaced_pool.tile([P, PIX, 2, P, 2], BF16, name="spaced")
+
+        def keep_warm(bank):
+            nc.tensor.matmul(out=bank, lhsT=ident_bf[:], rhs=zeros[:], start=True, stop=True)
+
+        def turn_pair(g, spaced, pair):
+            n_pix = min(2, PIX - 2 * pair)
             spaced_words = spaced[:].rearrange("b x u p e -> b (x u p e)").bitcast(F32)
-            for pair in range(PAIRS):
-                n_pix = min(2, PIX - 2 * pair)
-                planes = psum.tile([P, 2, 2, P], F32, tag="bank")
-                for e in range(n_pix):
-                    for u in range(2):
-                        word0 = P * (2 * (2 * pair + e) + u)
-                        nc.tensor.transpose(planes[:, e, u, :], spaced_words[:, word0 : word0 + P], ident_f32[:])
-                grouped = regroup.tile([P, 2 * P * PACK], BF16, align_bytes=64)
-                nc.scalar.copy(
-                    out=grouped[:, 0 : n_pix * P * PACK].bitcast(F32).rearrange("p (e b u) -> p e b u", b=P, u=2),
-                    in_=planes[:, 0:n_pix].rearrange("p e u b -> p e b u"),
-                )
-                cols_q = slice(2 * P * pair, 2 * P * pair + P * n_pix)
-                nc.vector.quantize_mx(
-                    out=fv_codes[g][:, cols_q].bitcast(FP8X4),
-                    scales=fv_scales[g][:, cols_q],
-                    in_=grouped[:, 0 : n_pix * P * PACK],
-                )
+            planes = psum.tile([P, 2, 2, P], F32, tag="bank")
+            if pair in WARM_PAIRS[g]:
+                keep_warm(planes[:].rearrange("p e u b -> p (e u b)"))
+            for e in range(n_pix):
+                for u in range(2):
+                    word0 = P * (2 * (2 * pair + e) + u)
+                    nc.tensor.transpose(planes[:, e, u, :], spaced_words[:, word0 : word0 + P], ident_f32[:])
+            grouped = regroup.tile([P, 2 * P * PACK], BF16, align_bytes=64)
+            nc.scalar.copy(
+                out=grouped[:, 0 : n_pix * P * PACK].bitcast(F32).rearrange("p (e b u) -> p e b u", b=P, u=2),
+                in_=planes[:, 0:n_pix].rearrange("p e u b -> p e b u"),
+            )
+            return grouped
+
+        def quantise_pair(g, grouped, pair):
+            n_pix = min(2, PIX - 2 * pair)
+            cols_q = slice(2 * P * pair, 2 * P * pair + P * n_pix)
+            nc.vector.quantize_mx(
+                out=fv_codes[g][:, cols_q].bitcast(FP8X4),
+                scales=fv_scales[g][:, cols_q],
+                in_=grouped[:, 0 : n_pix * P * PACK],
+            )
 
         col_slices = [slice(c, min(c + BANK, COLS)) for c in range(0, COLS, BANK)]
+        all_banks = list(range(len(col_slices)))
 
-        def multiply(t, accs, g, banks):
-            for k in banks:
-                width = col_slices[k].stop - col_slices[k].start
-                nc.tensor.matmul_mx(
-                    out=accs[k][:, 0:width],
-                    lhsT=w_words[g][:, 2 * P * t : 2 * P * (t + 1)].bitcast(FP4X4),
-                    lhsT_scale=w_scales[:, g, P * t : P * (t + 1)],
-                    rhs=fv_codes[g][:, col_slices[k]].bitcast(FP8X4),
-                    rhs_scale=fv_scales[g][:, col_slices[k]],
-                    start=(g == 0),
-                    stop=(g == PASSES - 1),
-                )
+        def multiply(t, acc, g, k):
+            width = col_slices[k].stop - col_slices[k].start
+            nc.tensor.matmul_mx(
+                out=acc[:, 0:width],
+                lhsT=w_words[g][:, 2 * P * t : 2 * P * (t + 1)].bitcast(FP4X4),
+                lhsT_scale=w_scales[:, g, P * t : P * (t + 1)],
+                rhs=fv_codes[g][:, col_slices[k]].bitcast(FP8X4),
+                rhs_scale=fv_scales[g][:, col_slices[k]],
+                start=(g == 0),
+                stop=(g == PASSES - 1),
+            )
 
-        def new_accs():
-            accs = []
-            for k in range(len(col_slices)):
-                acc = psum.tile([P, BANK], F32, tag="bank", name="acc")
-                accs.append(acc)
-            return accs
+        def new_acc():
+            acc = psum.tile([P, BANK], F32, tag="bank", name="acc")
+            return acc
 
-        def transpose_wfc(r):
-            wfc_t = psum.tile([P, k_tiles, P], BF16, tag="bank")
+        vec_tiles = []
+        gate_accs = []
+
+        def turn_vectors():
+            vec_t = psum.tile([P, P], BF16, tag="bank")
+            nc.tensor.transpose(vec_t[:], vec_rows[:], ident_bf[:])
+            vec_tiles.append(vec_t)
+
+        def col(v):
+            return cols[:, v, :]
+
+        def norm_1():
+            nc.vector.tensor_copy(
+                out=cols[:], in_=vec_tiles[0][:, 0 : len(vectors) * rows].rearrange("p (v r) -> p v r", r=rows)
+            )
+            nc.vector.tensor_scalar_add(out=std[:], in0=col(4), scalar1=EPS)
+            nc.vector.tensor_scalar_add(out=gate_bias[:], in0=col(5), scalar1=1.0)
+            nc.vector.tensor_sub(out=shift[:], in0=col(0), in1=col(3))
+
+        def norm_2():
+            nc.scalar.activation(out=std[:], in_=std[:], func=ACT.Sqrt)
+
+        def norm_3():
+            nc.vector.reciprocal(out=rstd[:], in_=std[:])
+            nc.vector.tensor_mul(out=scale[:], in0=col(1), in1=rstd[:])
+            nc.vector.tensor_mul(out=shift[:], in0=shift[:], in1=scale[:])
+            nc.vector.tensor_add(out=shift[:], in0=shift[:], in1=col(2))
+
+        def turn_ft():
+            ft_t = psum.tile([P, k_tiles, P], BF16, tag="bank")
             for kt in range(k_tiles):
-                nc.tensor.transpose(wfc_t[:, kt, :], wfc[r][:, P * kt : P * (kt + 1)], ident_bf[:])
-            nc.scalar.copy(out=wfcT[:, :, P * r : P * (r + 1)], in_=wfc_t[:])
+                nc.tensor.transpose(ft_t[:, kt, :], ft_sb[:, P * kt : P * (kt + 1)], ident_bf[:])
+            nc.scalar.copy(out=ftT[:], in_=ft_t[:])
 
-        def epilogue(t, accs):
-            normed = work.tile([P, COLS], F32, align_bytes=64)
-            for k, cs in enumerate(col_slices):
-                nc.scalar.activation(
-                    out=normed[:, cs],
-                    in_=accs[k][:, 0 : cs.stop - cs.start],
-                    func=ACT.Relu,
-                    scale=scale[:, t : t + 1],
-                    bias=shift[:, t : t + 1],
-                )
-            turned = work.tile([P, COLS], F32, align_bytes=64)
-            for cs in col_slices:
-                nc.vector.transpose(out=turned[:, cs], in_=normed[:, cs])
-            last = t == O_TILES - 1
-            by_three = work.tile([P, TRI, P, TRI], F32)
-            turned_g = turned[:].rearrange("p (g x n) -> p g n x", g=TRI, x=TRI)
-            if last:
-                for grp in range(TRI):
-                    nc.scalar.copy(out=by_three[:, grp], in_=turned_g[:, grp])
-            else:
-                nc.scalar.copy(out=by_three[:], in_=turned_g)
+        def turn_wfc(r):
+            def item():
+                wfc_t = psum.tile([P, k_tiles, P], BF16, tag="bank")
+                for kt in range(k_tiles):
+                    nc.tensor.transpose(wfc_t[:, kt, :], wfc[r][:, P * kt : P * (kt + 1)], ident_bf[:])
+                nc.scalar.copy(out=wfcT[:, :, P * r : P * (r + 1)], in_=wfc_t[:])
+
+            return item
+
+        def gate_part(t):
+            def item():
+                if t % PER_BANK == 0:
+                    gate_acc = psum.tile([P, PER_BANK, P], F32, tag="bank")
+                    gate_accs.append(gate_acc)
+                for kt in range(k_tiles):
+                    nc.tensor.matmul(
+                        out=gate_accs[-1][:, t % PER_BANK, :],
+                        lhsT=wfcT[:, kt, P * t : P * (t + 1)],
+                        rhs=ftT[:, kt, :],
+                        start=(kt == 0),
+                        stop=(kt == k_tiles - 1),
+                    )
+
+            return item
+
+        def gate_finish(half):
+            h_cols = slice(BANK * half, BANK * (half + 1))
+            nc.vector.tensor_add(
+                out=gate_o[:, h_cols].rearrange("p (q b) -> p q b", b=P),
+                in0=gate_accs[half][:],
+                in1=gate_bias[:, PER_BANK * half : PER_BANK * (half + 1)].unsqueeze(2).to_broadcast([P, PER_BANK, P]),
+            )
+            nc.vector.transpose(out=gate_t[:, h_cols], in_=gate_o[:, h_cols])
+
+        start_bank = psum.tile([P, BANK], F32, tag="bank")
+        for i in range(WARM_START):
+            keep_warm(start_bank[:])
+        accs0 = [new_acc() for k in all_banks]
+
+        def early(g):
+            def item():
+                for k in all_banks:
+                    multiply(0, accs0[k], g, k)
+
+            return item
+
+        woven = [
+            {4: [turn_vectors]},
+            {1: [norm_1], 2: [turn_ft], 3: [turn_wfc(0)], 4: [turn_wfc(1)]},
+            {0: [norm_2], 1: [turn_wfc(2)], 3: [turn_wfc(3)], 4: [gate_part(0), gate_part(1)]},
+            {0: [norm_3], 1: [gate_part(2), gate_part(3)], 2: [turn_wfc(4)], 3: [early(0)], 4: [turn_wfc(5), early(1)]},
+            {1: [turn_wfc(6), early(2)], 2: [turn_wfc(7)], 3: [gate_part(4), gate_part(5)]},
+            {1: [early(3)], 3: [gate_part(6), gate_part(7)]},
+        ]
+        sorts_before = (2, 1, 1, 0, 0)
+        spaced = new_spaced()
+        calls, call_last = sort_parts(0, spaced)
+        call_last()
+        for call in calls:
+            call()
+        for g in range(PASSES):
+            calls = []
+            if g + 1 < PASSES:
+                next_spaced = new_spaced()
+                calls, call_last = sort_parts(g + 1, next_spaced)
+            done = 0
+            for pair in range(PAIRS):
+                for call in calls[done : done + sorts_before[pair]]:
+                    call()
+                done += sorts_before[pair]
+                grouped = turn_pair(g, spaced, pair)
+                if pair == 1 and calls:
+                    call_last()
+                quantise_pair(g, grouped, pair)
+                for work_item in woven[g].get(pair, []):
+                    work_item()
+            spaced = next_spaced
+        gate_finish(0)
+        early(4)()
+        early(5)()
+
+        def normalise(t, k, acc, normed):
+            cs = col_slices[k]
+            nc.scalar.activation(
+                out=normed[:, cs],
+                in_=acc[:, 0 : cs.stop - cs.start],
+                func=ACT.Relu,
+                scale=scale[:, t : t + 1],
+                bias=shift[:, t : t + 1],
+            )
+
+        def turn_squares(k, normed, turned):
+            nc.vector.transpose(out=turned[:, col_slices[k]], in_=normed[:, col_slices[k]])
+
+        def interleave(turned, by_three, groups):
+            nc.scalar.copy(
+                out=by_three[:, groups],
+                in_=turned[:].rearrange("p (g x n) -> p g n x", g=TRI, x=TRI)[:, groups],
+            )
+
+        def gate_and_store(t, by_three, parts):
             result = store_pool.tile([P, P, PIX], F32)
-            parts = 2 if last else 1
             blks = BLKS // parts
             for part in range(parts):
                 n_s = slice(P // parts * part, P // parts * (part + 1))
@@ -227,84 +359,29 @@ def tile_joint_module_pa_kernel(
                         in_=result[SQ * i : SQ * (i + 1), n_s].rearrange("c (j r) x -> c j (r x)", j=blks),
                     )
 
-        def text_gate(half):
-            gate_acc = psum.tile([P, PER_BANK, P], F32, tag="bank")
-            for q in range(PER_BANK):
-                t = PER_BANK * half + q
-                for kt in range(k_tiles):
-                    nc.tensor.matmul(
-                        out=gate_acc[:, q, :],
-                        lhsT=wfcT[:, kt, P * t : P * (t + 1)],
-                        rhs=ftT[:, kt, :],
-                        start=(kt == 0),
-                        stop=(kt == k_tiles - 1),
-                    )
-            h_cols = slice(BANK * half, BANK * (half + 1))
-            nc.vector.tensor_add(
-                out=gate_o[:, h_cols].rearrange("p (q b) -> p q b", b=P),
-                in0=gate_acc[:],
-                in1=gate_bias[:, PER_BANK * half : PER_BANK * (half + 1)].unsqueeze(2).to_broadcast([P, PER_BANK, P]),
-            )
-            nc.vector.transpose(out=gate_t[:, h_cols], in_=gate_o[:, h_cols])
-
-        all_banks = list(range(len(col_slices)))
-        early_banks = all_banks[0:2]
-        accs0 = new_accs()
-        accs1 = []
-        for k in early_banks:
-            acc = psum.tile([P, BANK], F32, tag="bank", name="acc")
-            accs1.append(acc)
-
-        def early_passes(g):
-            multiply(0, accs0, g, all_banks)
-            multiply(1, accs1, g, early_banks)
-
-        for g in range(PASSES):
-            spaced = sort_by_pixel(g)
-            quantise(g, spaced)
-            if g == 2:
-                early_passes(0)
-            if g >= 2:
-                early_passes(g - 1)
-            if g == 3:
-                vec_t = psum.tile([P, P], BF16, tag="bank")
-                nc.tensor.transpose(vec_t[:], vec_rows[:], ident_bf[:])
-                nc.vector.tensor_copy(
-                    out=cols[:], in_=vec_t[:, 0 : len(vectors) * rows].rearrange("p (v r) -> p v r", r=rows)
-                )
-                col_b1, col_g1, col_be1, col_m1, col_v1, col_bfc1 = [cols[:, v, :] for v in range(len(vectors))]
-                nc.vector.tensor_scalar_add(out=std[:], in0=col_v1, scalar1=EPS)
-                nc.scalar.activation(out=std[:], in_=std[:], func=ACT.Sqrt)
-                nc.vector.reciprocal(out=rstd[:], in_=std[:])
-                nc.vector.tensor_mul(out=scale[:], in0=col_g1, in1=rstd[:])
-                nc.vector.tensor_sub(out=shift[:], in0=col_b1, in1=col_m1)
-                nc.vector.tensor_mul(out=shift[:], in0=shift[:], in1=scale[:])
-                nc.vector.tensor_add(out=shift[:], in0=shift[:], in1=col_be1)
-                nc.vector.tensor_scalar_add(out=gate_bias[:], in0=col_bfc1, scalar1=1.0)
-                ft_t = psum.tile([P, k_tiles, P], BF16, tag="bank")
-                for kt in range(k_tiles):
-                    nc.tensor.transpose(ft_t[:, kt, :], ft_sb[:, P * kt : P * (kt + 1)], ident_bf[:])
-                nc.scalar.copy(out=ftT[:], in_=ft_t[:])
-            if g == 4:
-                for r in range(rows // 2):
-                    transpose_wfc(r)
-        text_gate(0)
-        early_passes(PASSES - 1)
-        epilogue(0, accs0)
-
-        for t in range(1, O_TILES):
-            if t == 1:
-                acc = psum.tile([P, BANK], F32, tag="bank", name="acc")
-                accs = accs1 + [acc]
-                todo = all_banks[2:]
-            else:
-                accs = new_accs()
-                todo = all_banks
-            for k in todo:
-                for g in range(PASSES):
-                    multiply(t, accs, g, [k])
-            epilogue(t, accs)
-            if t == 1:
-                for r in range(rows // 2, rows):
-                    transpose_wfc(r)
-                text_gate(1)
+        every_group = slice(0, TRI)
+        before = None
+        for t in range(O_TILES):
+            last = t == O_TILES - 1
+            normed = work.tile([P, COLS], F32, align_bytes=64)
+            turned = work.tile([P, COLS], F32, align_bytes=64)
+            by_three = work.tile([P, TRI, P, TRI], F32)
+            for k in all_banks:
+                if t == 0:
+                    acc = accs0[k]
+                else:
+                    acc = new_acc()
+                    for g in range(PASSES):
+                        multiply(t, acc, g, k)
+                normalise(t, k, acc, normed)
+                turn_squares(k, normed, turned)
+                if k == 0 and before:
+                    interleave(before[0], before[1], every_group)
+                    gate_and_store(t - 1, before[1], 1)
+                    if t == 1:
+                        gate_finish(1)
+                if last and k > 0:
+                    interleave(turned, by_three, slice(k - 1, k))
+            before = (turned, by_three)
+        interleave(before[0], before[1], slice(TRI - 1, TRI))
+        gate_and_store(O_TILES - 1, before[1], 2)

@@ -28,6 +28,7 @@ O_TILES = C_OUT // P
 SQ = 32
 BLKS = P // SQ
 FIRST_PARTS = 2
+SCALAR_SORTS = (0, 1)
 PER_BANK = BANK // P
 WARM_START = 6
 WARM_PAIRS = ((0, 1, 2, 3, 4), (0, 2, 4), (), (), (), ())
@@ -103,13 +104,13 @@ def tile_joint_module_pa_kernel(
                 nc.sync.dma_start(out=wfc[r][:], in_=Wfc1[P * r : P * (r + 1), :])
 
         load_fv(0, FIRST_PARTS)
+        load_fv(1, FIRST_PARTS)
+        load_fv(2)
         for v, vector in enumerate(vectors):
             nc.sync.dma_start(
                 out=vec_rows[rows * v : rows * (v + 1), :],
                 in_=vector.rearrange("(r c) -> r c", c=P),
             )
-        load_fv(1)
-        load_fv(2)
         nc.sync.dma_start(out=ft_sb[:], in_=ft)
         load_wfc(0, rows // 2)
         load_fv(3)
@@ -146,14 +147,14 @@ def tile_joint_module_pa_kernel(
                     out=spaced[:, PIX - 1].rearrange("b u p e -> b p u e"), in_=by_channel[:, :, :, :, PIX - 1]
                 )
 
-            parts = FIRST_PARTS if g == 0 else 1
+            parts = FIRST_PARTS if g < 2 else 1
             calls = []
             for part in range(parts):
                 p_s = slice(P // parts * part, P // parts * (part + 1))
                 for x0 in range(0, PIX - 1, 4):
                     for u in range(2):
                         calls.append(four(x0, u, p_s))
-            return calls, last_pixel(nc.scalar.copy)
+            return calls, last_pixel(nc.scalar.copy if g in SCALAR_SORTS else nc.vector.tensor_copy)
 
         def new_spaced():
             return spaced_pool.tile([P, PIX, 2, P, 2], BF16, name="spaced")
@@ -287,12 +288,12 @@ def tile_joint_module_pa_kernel(
             return item
 
         woven = [
-            {4: [turn_vectors]},
-            {1: [norm_1], 2: [turn_ft], 3: [turn_wfc(0)], 4: [turn_wfc(1)]},
-            {0: [norm_2], 1: [turn_wfc(2)], 3: [turn_wfc(3)], 4: [gate_part(0), gate_part(1)]},
-            {0: [norm_3], 1: [gate_part(2), gate_part(3)], 2: [turn_wfc(4)], 3: [early(0)], 4: [turn_wfc(5), early(1)]},
-            {1: [turn_wfc(6), early(2)], 2: [turn_wfc(7)], 3: [gate_part(4), gate_part(5)]},
-            {1: [early(3)], 3: [gate_part(6), gate_part(7)]},
+            {},
+            {0: [turn_vectors], 2: [turn_ft], 3: [turn_wfc(0)], 4: [turn_wfc(1)]},
+            {0: [norm_1], 1: [turn_wfc(2)], 3: [turn_wfc(3)]},
+            {0: [norm_2, gate_part(0)], 1: [gate_part(1)], 2: [turn_wfc(4)], 3: [gate_part(2), early(0)], 4: [turn_wfc(5), gate_part(3)]},
+            {0: [norm_3, early(1)], 1: [turn_wfc(6)], 2: [turn_wfc(7)], 3: [gate_part(4), early(2)], 4: [gate_part(5)]},
+            {1: [early(3)], 2: [gate_part(6)], 3: [gate_part(7)]},
         ]
         sorts_before = (2, 1, 1, 0, 0)
         spaced = new_spaced()
@@ -307,9 +308,10 @@ def tile_joint_module_pa_kernel(
                 calls, call_last = sort_parts(g + 1, next_spaced)
             done = 0
             for pair in range(PAIRS):
-                for call in calls[done : done + sorts_before[pair]]:
+                share = sorts_before[pair] * (len(calls) // 4)
+                for call in calls[done : done + share]:
                     call()
-                done += sorts_before[pair]
+                done += share
                 grouped = turn_pair(g, spaced, pair)
                 if pair == 1 and calls:
                     call_last()
@@ -334,10 +336,10 @@ def tile_joint_module_pa_kernel(
         def turn_squares(k, normed, turned):
             nc.vector.transpose(out=turned[:, col_slices[k]], in_=normed[:, col_slices[k]])
 
-        def interleave(turned, by_three, groups):
+        def interleave(turned, by_three, grp):
             nc.scalar.copy(
-                out=by_three[:, groups],
-                in_=turned[:].rearrange("p (g x n) -> p g n x", g=TRI, x=TRI)[:, groups],
+                out=by_three[:, grp],
+                in_=turned[:].rearrange("p (g x n) -> p g n x", g=TRI, x=TRI)[:, grp],
             )
 
         def gate_and_store(t, by_three, parts):
@@ -359,10 +361,7 @@ def tile_joint_module_pa_kernel(
                         in_=result[SQ * i : SQ * (i + 1), n_s].rearrange("c (j r) x -> c j (r x)", j=blks),
                     )
 
-        every_group = slice(0, TRI)
-        before = None
         for t in range(O_TILES):
-            last = t == O_TILES - 1
             normed = work.tile([P, COLS], F32, align_bytes=64)
             turned = work.tile([P, COLS], F32, align_bytes=64)
             by_three = work.tile([P, TRI, P, TRI], F32)
@@ -375,13 +374,12 @@ def tile_joint_module_pa_kernel(
                         multiply(t, acc, g, k)
                 normalise(t, k, acc, normed)
                 turn_squares(k, normed, turned)
-                if k == 0 and before:
-                    interleave(before[0], before[1], every_group)
-                    gate_and_store(t - 1, before[1], 1)
-                    if t == 1:
-                        gate_finish(1)
-                if last and k > 0:
-                    interleave(turned, by_three, slice(k - 1, k))
-            before = (turned, by_three)
-        interleave(before[0], before[1], slice(TRI - 1, TRI))
-        gate_and_store(O_TILES - 1, before[1], 2)
+                if t > 0 and k == (0 if t == O_TILES - 1 else len(all_banks) - 1):
+                    gate_and_store(t - 1, before, 1)
+                if k > 0:
+                    interleave(turned, by_three, k - 1)
+            interleave(turned, by_three, TRI - 1)
+            before = by_three
+            if t == 0:
+                gate_finish(1)
+        gate_and_store(O_TILES - 1, before, 2)

@@ -356,7 +356,8 @@ def tile_joint_module_pa_kernel(
                 for i in range(BLKS):
                     o_lo = P * t + SQ * i
                     by_block = out_rows[SQ * blks * part : SQ * blks * (part + 1), PIX * o_lo : PIX * (o_lo + SQ)]
-                    nc.sync.dma_start(
+                    queue = nc.sync if i < BLKS // 2 else (nc.scalar if t == O_TILES - 1 else nc.gpsimd)
+                    queue.dma_start(
                         out=by_block.rearrange("(j c) n -> c j n", c=SQ),
                         in_=result[SQ * i : SQ * (i + 1), n_s].rearrange("c (j r) x -> c j (r x)", j=blks),
                     )

@@ -31,7 +31,7 @@ FIRST_PARTS = 2
 SCALAR_SORTS = (0, 1)
 PER_BANK = BANK // P
 WARM_START = 6
-WARM_PAIRS = ((0, 1, 2, 3, 4), (0, 2, 4), (), (), (), ())
+WARM_PAIRS = ((0, 1, 2, 3, 4), (0, 1, 2), (0,), (), (), ())
 TRI = 3
 
 FLOPS = 2 * P * PIX * C_IN * C_OUT + 2 * P * C_TXT * C_OUT
@@ -105,24 +105,27 @@ def tile_joint_module_pa_kernel(
 
         load_fv(0, FIRST_PARTS)
         load_fv(1, FIRST_PARTS)
+        nc.sync.dma_start(out=ft_sb[:], in_=ft)
+        load_wfc(0, 2)
         load_fv(2)
         for v, vector in enumerate(vectors):
             nc.sync.dma_start(
                 out=vec_rows[rows * v : rows * (v + 1), :],
                 in_=vector.rearrange("(r c) -> r c", c=P),
             )
-        nc.sync.dma_start(out=ft_sb[:], in_=ft)
-        load_wfc(0, rows // 2)
+        load_wfc(2, 4)
         load_fv(3)
         for quad in range(4):
             nc.sync.dma_start(
                 out=w_scales[32 * quad : 32 * quad + 4].bitcast(I32),
                 in_=W1_scales[:, 4 * quad : 4 * quad + 4, :].rearrange("g r n -> r g n").bitcast(I32),
             )
-        for g in range(3):
-            load_words(g)
+        load_words(0)
+        load_words(1)
+        load_wfc(4, 6)
         load_fv(4)
-        load_wfc(rows // 2, rows)
+        load_wfc(6, 8)
+        load_words(2)
         load_fv(5)
         for g in range(3, PASSES):
             load_words(g)
@@ -288,12 +291,12 @@ def tile_joint_module_pa_kernel(
             return item
 
         woven = [
-            {},
-            {0: [turn_vectors], 2: [turn_ft], 3: [turn_wfc(0)], 4: [turn_wfc(1)]},
-            {0: [norm_1], 1: [turn_wfc(2)], 3: [turn_wfc(3)]},
-            {0: [norm_2, gate_part(0)], 1: [gate_part(1)], 2: [turn_wfc(4)], 3: [gate_part(2), early(0)], 4: [turn_wfc(5), gate_part(3)]},
-            {0: [norm_3, early(1)], 1: [turn_wfc(6)], 2: [turn_wfc(7)], 3: [gate_part(4), early(2)], 4: [gate_part(5)]},
-            {1: [early(3)], 2: [gate_part(6)], 3: [gate_part(7)]},
+            {4: [turn_ft]},
+            {3: [turn_wfc(0)], 4: [turn_wfc(1)]},
+            {0: [turn_vectors], 1: [turn_wfc(2)], 2: [gate_part(0), norm_1], 3: [turn_wfc(3)], 4: [gate_part(1)]},
+            {0: [norm_2], 1: [gate_part(2)], 2: [turn_wfc(4)], 3: [gate_part(3), early(0)], 4: [turn_wfc(5)]},
+            {0: [norm_3], 1: [gate_part(4), early(1)], 2: [turn_wfc(6)], 3: [gate_part(5)], 4: [turn_wfc(7)]},
+            {1: [early(2), gate_part(6)], 3: [early(3), gate_part(7)]},
         ]
         sorts_before = (2, 1, 1, 0, 0)
         spaced = new_spaced()
@@ -336,8 +339,8 @@ def tile_joint_module_pa_kernel(
         def turn_squares(k, normed, turned):
             nc.vector.transpose(out=turned[:, col_slices[k]], in_=normed[:, col_slices[k]])
 
-        def interleave(turned, by_three, grp):
-            nc.scalar.copy(
+        def interleave(copy, turned, by_three, grp):
+            copy(
                 out=by_three[:, grp],
                 in_=turned[:].rearrange("p (g x n) -> p g n x", g=TRI, x=TRI)[:, grp],
             )
@@ -366,6 +369,7 @@ def tile_joint_module_pa_kernel(
             normed = work.tile([P, COLS], F32, align_bytes=64)
             turned = work.tile([P, COLS], F32, align_bytes=64)
             by_three = work.tile([P, TRI, P, TRI], F32)
+            copy = nc.scalar.copy if t < O_TILES - 1 else nc.vector.tensor_copy
             for k in all_banks:
                 if t == 0:
                     acc = accs0[k]
@@ -374,12 +378,14 @@ def tile_joint_module_pa_kernel(
                     for g in range(PASSES):
                         multiply(t, acc, g, k)
                 normalise(t, k, acc, normed)
+                if t == O_TILES - 1 and k == 0:
+                    gate_and_store(t - 1, before, 1)
                 turn_squares(k, normed, turned)
-                if t > 0 and k == (0 if t == O_TILES - 1 else len(all_banks) - 1):
+                if 0 < t < O_TILES - 1 and k == len(all_banks) - 1:
                     gate_and_store(t - 1, before, 1)
                 if k > 0:
-                    interleave(turned, by_three, k - 1)
-            interleave(turned, by_three, TRI - 1)
+                    interleave(copy, turned, by_three, k - 1)
+            interleave(copy, turned, by_three, TRI - 1)
             before = by_three
             if t == 0:
                 gate_finish(1)

@@ -28,7 +28,6 @@ O_TILES = C_OUT // P
 SQ = 32
 BLKS = P // SQ
 FIRST_PARTS = 2
-SCALAR_SORTS = (0, 1)
 PER_BANK = BANK // P
 WARM_START = 6
 WARM_PAIRS = ((0, 1, 2, 3, 4), (0, 1, 2), (0,), (), (), ())
@@ -141,8 +140,8 @@ def tile_joint_module_pa_kernel(
 
             def four(x0, u, p_s):
                 return lambda: nc.vector.tensor_copy(
-                    out=spaced[:, x0 : x0 + 4, u, p_s, :].rearrange("b (h x) p e -> b h p e x", h=2),
-                    in_=by_channel[:, p_s, u, :, x0 : x0 + 4].rearrange("b p e (h x) -> b h p e x", h=2),
+                    out=spaced[:, x0 : x0 + 4, u, p_s, :].rearrange("b (h x) p e -> b h p x e", h=2),
+                    in_=by_channel[:, p_s, u, :, x0 : x0 + 4].rearrange("b p e (h x) -> b h p x e", h=2),
                 )
 
             def last_pixel(copy):
@@ -157,7 +156,7 @@ def tile_joint_module_pa_kernel(
                 for x0 in range(0, PIX - 1, 4):
                     for u in range(2):
                         calls.append(four(x0, u, p_s))
-            return calls, last_pixel(nc.scalar.copy if g in SCALAR_SORTS else nc.vector.tensor_copy)
+            return calls, last_pixel(nc.scalar.copy)
 
         def new_spaced():
             return spaced_pool.tile([P, PIX, 2, P, 2], BF16, name="spaced")

from contextlib import ExitStack

import concourse.mybir as mybir
from concourse.masks import make_identity

F32 = mybir.dt.float32
BF16 = mybir.dt.bfloat16
I32 = mybir.dt.int32
U32 = mybir.dt.uint32
U8 = mybir.dt.uint8
FP8X4 = mybir.dt.float8_e4m3fn_x4
FP4X4 = mybir.dt.float4_e2m1fn_x4
ACT = mybir.ActivationFunctionType

P = 128
C_IN = 3072
C_OUT = 1024
C_TXT = 1024
PIX = 9
EPS = 1e-5
PACK = 4
K_PASS = P * PACK
PASSES = C_IN // K_PASS
PAIRS = (PIX + 1) // 2
BANK = 512
COLS = PIX * P
O_TILES = C_OUT // P
SQ = 32
BLKS = P // SQ
FIRST_PARTS = 2
PER_BANK = BANK // P
WARM_START = 6
WARM_PAIRS = ((0, 1, 2, 3, 4), (0, 1, 2), (0,), (), (), ())
TRI = 3

FLOPS = 2 * P * PIX * C_IN * C_OUT + 2 * P * C_TXT * C_OUT


def tile_joint_module_pa_kernel(
    tc, fv, ft, W1_words, W1_scales, b1, g1, be1, m1, v1, Wfc1, bfc1, out
):
    nc = tc.nc
    fv_rows = fv.rearrange("b c h w -> b (c h w)")
    out_rows = out.rearrange("b o h w -> b (o h w)")
    chunk = K_PASS * PIX

    with ExitStack() as ctx:
        keep = ctx.enter_context(tc.tile_pool(name="keep", bufs=1))
        psum = ctx.enter_context(tc.psum_pool(name="psum", bufs=8))
        spaced_pool = ctx.enter_context(tc.tile_pool(name="spaced", bufs=3))
        regroup = ctx.enter_context(tc.tile_pool(name="regroup", bufs=6))
        work = ctx.enter_context(tc.tile_pool(name="work", bufs=2))
        store_pool = ctx.enter_context(tc.tile_pool(name="store", bufs=3))

        vectors = [b1, g1, be1, m1, v1, bfc1]
        rows = C_OUT // P
        k_tiles = C_TXT // P

        w_words = [keep.tile([P, 2 * C_OUT], U8, align_bytes=64, name="w_words%d" % g) for g in range(PASSES)]
        w_scales = keep.tile([P, PASSES, C_OUT], U8, align_bytes=64)
        fv_codes = [keep.tile([P, COLS], U32, align_bytes=64, name="fv_codes%d" % g) for g in range(PASSES)]
        fv_scales = [keep.tile([P, COLS], U8, align_bytes=64, name="fv_scales%d" % g) for g in range(PASSES)]
        fv_sb = [keep.tile([P, chunk], BF16, name="fv_sb%d" % g) for g in range(PASSES)]
        ft_sb = keep.tile([P, C_TXT], BF16)
        wfc = [keep.tile([P, C_TXT], BF16, name="wfc%d" % r) for r in range(rows)]
        cols = keep.tile([P, len(vectors), rows], F32)
        std = keep.tile([P, rows], F32)
        rstd = keep.tile([P, rows], F32)
        scale = keep.tile([P, rows], F32)
        shift = keep.tile([P, rows], F32)
        gate_bias = keep.tile([P, rows], F32)
        ftT = keep.tile([P, k_tiles, P], BF16)
        wfcT = keep.tile([P, k_tiles, C_OUT], BF16)
        gate_o = keep.tile([P, O_TILES * P], F32, align_bytes=64)
        gate_t = keep.tile([P, O_TILES * P], F32, align_bytes=64)

        ident_f32 = keep.tile([P, P], F32)
        make_identity(nc, ident_f32[:])
        ident_bf = keep.tile([P, P], BF16)
        make_identity(nc, ident_bf[:])
        nc.gpsimd.memset(w_scales[:].rearrange("p g n -> p (g n)").bitcast(I32), 0)
        vec_rows = keep.tile([P, P], BF16)
        nc.vector.memset(vec_rows[:], 0.0)
        zeros = keep.tile([P, BANK], BF16)
        nc.vector.memset(zeros[:], 0.0)

        warm = keep.tile([P, 1], F32)
        nc.vector.memset(warm[:], 1.0)
        nc.scalar.activation(out=warm[:], in_=warm[:], func=ACT.Sqrt)

        def load_fv(g, parts=1):
            step = chunk // parts
            for lo in range(0, chunk, step):
                nc.sync.dma_start(
                    out=fv_sb[g][:, lo : lo + step], in_=fv_rows[:, chunk * g + lo : chunk * g + lo + step]
                )

        def load_words(g):
            nc.sync.dma_start(out=w_words[g][:].bitcast(I32), in_=W1_words[g].bitcast(I32))

        def load_wfc(r_lo, r_hi):
            for r in range(r_lo, r_hi):
                nc.sync.dma_start(out=wfc[r][:], in_=Wfc1[P * r : P * (r + 1), :])

        load_fv(0, FIRST_PARTS)
        load_fv(1, FIRST_PARTS)
        nc.sync.dma_start(out=ft_sb[:], in_=ft)
        load_wfc(0, 2)
        load_fv(2)
        for v, vector in enumerate(vectors):
            nc.sync.dma_start(
                out=vec_rows[rows * v : rows * (v + 1), :],
                in_=vector.rearrange("(r c) -> r c", c=P),
            )
        load_wfc(2, 4)
        load_fv(3)
        for quad in range(4):
            nc.sync.dma_start(
                out=w_scales[32 * quad : 32 * quad + 4].bitcast(I32),
                in_=W1_scales[:, 4 * quad : 4 * quad + 4, :].rearrange("g r n -> r g n").bitcast(I32),
            )
        load_words(0)
        load_words(1)
        load_wfc(4, 6)
        load_fv(4)
        load_wfc(6, 8)
        load_words(2)
        load_fv(5)
        for g in range(3, PASSES):
            load_words(g)

        ctx.enter_context(
            tc.manual_schedule(
                engines={mybir.EngineType.PE, mybir.EngineType.DVE, mybir.EngineType.Activation}
            )
        )

        def sort_parts(g, spaced):
            by_channel = fv_sb[g][:].rearrange("b (p u e x) -> b p u e x", u=2, e=2, x=PIX)

            def four(x0, u, p_s):
                return lambda: nc.vector.tensor_copy(
                    out=spaced[:, x0 : x0 + 4, u, p_s, :].rearrange("b (h x) p e -> b h p x e", h=2),
                    in_=by_channel[:, p_s, u, :, x0 : x0 + 4].rearrange("b p e (h x) -> b h p x e", h=2),
                )

            def last_pixel(copy):
                return lambda: copy(
                    out=spaced[:, PIX - 1].rearrange("b u p e -> b p u e"), in_=by_channel[:, :, :, :, PIX - 1]
                )

            parts = FIRST_PARTS if g < 2 else 1
            calls = []
            for part in range(parts):
                p_s = slice(P // parts * part, P // parts * (part + 1))
                for x0 in range(0, PIX - 1, 4):
                    for u in range(2):
                        calls.append(four(x0, u, p_s))
            return calls, last_pixel(nc.scalar.copy)

        def new_spaced():
            return spaced_pool.tile([P, PIX, 2, P, 2], BF16, name="spaced")

        def keep_warm(bank):
            nc.tensor.matmul(out=bank, lhsT=ident_bf[:], rhs=zeros[:], start=True, stop=True)

        def turn_pair(g, spaced, pair):
            n_pix = min(2, PIX - 2 * pair)
            spaced_words = spaced[:].rearrange("b x u p e -> b (x u p e)").bitcast(F32)
            planes = psum.tile([P, 2, 2, P], F32, tag="bank")
            if pair in WARM_PAIRS[g]:
                keep_warm(planes[:].rearrange("p e u b -> p (e u b)"))
            for e in range(n_pix):
                for u in range(2):
                    word0 = P * (2 * (2 * pair + e) + u)
                    nc.tensor.transpose(planes[:, e, u, :], spaced_words[:, word0 : word0 + P], ident_f32[:])
            grouped = regroup.tile([P, 2 * P * PACK], BF16, align_bytes=64)
            nc.scalar.copy(
                out=grouped[:, 0 : n_pix * P * PACK].bitcast(F32).rearrange("p (e b u) -> p e b u", b=P, u=2),
                in_=planes[:, 0:n_pix].rearrange("p e u b -> p e b u"),
            )
            return grouped

        def quantise_pair(g, grouped, pair):
            n_pix = min(2, PIX - 2 * pair)
            cols_q = slice(2 * P * pair, 2 * P * pair + P * n_pix)
            nc.vector.quantize_mx(
                out=fv_codes[g][:, cols_q].bitcast(FP8X4),
                scales=fv_scales[g][:, cols_q],
                in_=grouped[:, 0 : n_pix * P * PACK],
            )

        col_slices = [slice(c, min(c + BANK, COLS)) for c in range(0, COLS, BANK)]
        all_banks = list(range(len(col_slices)))

        def multiply(t, acc, g, k):
            width = col_slices[k].stop - col_slices[k].start
            nc.tensor.matmul_mx(
                out=acc[:, 0:width],
                lhsT=w_words[g][:, 2 * P * t : 2 * P * (t + 1)].bitcast(FP4X4),
                lhsT_scale=w_scales[:, g, P * t : P * (t + 1)],
                rhs=fv_codes[g][:, col_slices[k]].bitcast(FP8X4),
                rhs_scale=fv_scales[g][:, col_slices[k]],
                start=(g == 0),
                stop=(g == PASSES - 1),
            )

        def new_acc():
            acc = psum.tile([P, BANK], F32, tag="bank", name="acc")
            return acc

        vec_tiles = []
        gate_accs = []

        def turn_vectors():
            vec_t = psum.tile([P, P], BF16, tag="bank")
            nc.tensor.transpose(vec_t[:], vec_rows[:], ident_bf[:])
            vec_tiles.append(vec_t)

        def col(v):
            return cols[:, v, :]

        def norm_1():
            nc.vector.tensor_copy(
                out=cols[:], in_=vec_tiles[0][:, 0 : len(vectors) * rows].rearrange("p (v r) -> p v r", r=rows)
            )
            nc.vector.tensor_scalar_add(out=std[:], in0=col(4), scalar1=EPS)
            nc.vector.tensor_scalar_add(out=gate_bias[:], in0=col(5), scalar1=1.0)
            nc.vector.tensor_sub(out=shift[:], in0=col(0), in1=col(3))

        def norm_2():
            nc.scalar.activation(out=std[:], in_=std[:], func=ACT.Sqrt)

        def norm_3():
            nc.vector.reciprocal(out=rstd[:], in_=std[:])
            nc.vector.tensor_mul(out=scale[:], in0=col(1), in1=rstd[:])
            nc.vector.tensor_mul(out=shift[:], in0=shift[:], in1=scale[:])
            nc.vector.tensor_add(out=shift[:], in0=shift[:], in1=col(2))

        def turn_ft():
            ft_t = psum.tile([P, k_tiles, P], BF16, tag="bank")
            for kt in range(k_tiles):
                nc.tensor.transpose(ft_t[:, kt, :], ft_sb[:, P * kt : P * (kt + 1)], ident_bf[:])
            nc.scalar.copy(out=ftT[:], in_=ft_t[:])

        def turn_wfc(r):
            def item():
                wfc_t = psum.tile([P, k_tiles, P], BF16, tag="bank")
                for kt in range(k_tiles):
                    nc.tensor.transpose(wfc_t[:, kt, :], wfc[r][:, P * kt : P * (kt + 1)], ident_bf[:])
                nc.scalar.copy(out=wfcT[:, :, P * r : P * (r + 1)], in_=wfc_t[:])

            return item

        def gate_part(t):
            def item():
                if t % PER_BANK == 0:
                    gate_acc = psum.tile([P, PER_BANK, P], F32, tag="bank")
                    gate_accs.append(gate_acc)
                for kt in range(k_tiles):
                    nc.tensor.matmul(
                        out=gate_accs[-1][:, t % PER_BANK, :],
                        lhsT=wfcT[:, kt, P * t : P * (t + 1)],
                        rhs=ftT[:, kt, :],
                        start=(kt == 0),
                        stop=(kt == k_tiles - 1),
                    )

            return item

        def gate_finish(half):
            h_cols = slice(BANK * half, BANK * (half + 1))
            nc.vector.tensor_add(
                out=gate_o[:, h_cols].rearrange("p (q b) -> p q b", b=P),
                in0=gate_accs[half][:],
                in1=gate_bias[:, PER_BANK * half : PER_BANK * (half + 1)].unsqueeze(2).to_broadcast([P, PER_BANK, P]),
            )
            nc.vector.transpose(out=gate_t[:, h_cols], in_=gate_o[:, h_cols])

        start_bank = psum.tile([P, BANK], F32, tag="bank")
        for i in range(WARM_START):
            keep_warm(start_bank[:])
        accs0 = [new_acc() for k in all_banks]

        def early(g):
            def item():
                for k in all_banks:
                    multiply(0, accs0[k], g, k)

            return item

        woven = [
            {4: [turn_ft]},
            {3: [turn_wfc(0)], 4: [turn_wfc(1)]},
            {0: [turn_vectors], 1: [turn_wfc(2)], 2: [gate_part(0), norm_1], 3: [turn_wfc(3)], 4: [gate_part(1)]},
            {0: [norm_2], 1: [gate_part(2)], 2: [turn_wfc(4)], 3: [gate_part(3), early(0)], 4: [turn_wfc(5)]},
            {0: [norm_3], 1: [gate_part(4), early(1)], 2: [turn_wfc(6)], 3: [gate_part(5)], 4: [turn_wfc(7)]},
            {1: [early(2), gate_part(6)], 3: [early(3), gate_part(7)]},
        ]
        sorts_before = (2, 1, 1, 0, 0)
        spaced = new_spaced()
        calls, call_last = sort_parts(0, spaced)
        call_last()
        for call in calls:
            call()
        for g in range(PASSES):
            calls = []
            if g + 1 < PASSES:
                next_spaced = new_spaced()
                calls, call_last = sort_parts(g + 1, next_spaced)
            done = 0
            for pair in range(PAIRS):
                share = sorts_before[pair] * (len(calls) // 4)
                for call in calls[done : done + share]:
                    call()
                done += share
                grouped = turn_pair(g, spaced, pair)
                if pair == 1 and calls:
                    call_last()
                quantise_pair(g, grouped, pair)
                for work_item in woven[g].get(pair, []):
                    work_item()
            spaced = next_spaced
        gate_finish(0)
        early(4)()
        early(5)()

        def normalise(t, k, acc, normed):
            cs = col_slices[k]
            nc.scalar.activation(
                out=normed[:, cs],
                in_=acc[:, 0 : cs.stop - cs.start],
                func=ACT.Relu,
                scale=scale[:, t : t + 1],
                bias=shift[:, t : t + 1],
            )

        def turn_squares(k, normed, turned):
            nc.vector.transpose(out=turned[:, col_slices[k]], in_=normed[:, col_slices[k]])

        def interleave(copy, turned, by_three, grp):
            copy(
                out=by_three[:, grp],
                in_=turned[:].rearrange("p (g x n) -> p g n x", g=TRI, x=TRI)[:, grp],
            )

        def gate_and_store(t, by_three, parts):
            result = store_pool.tile([P, P, PIX], F32)
            blks = BLKS // parts
            for part in range(parts):
                n_s = slice(P // parts * part, P // parts * (part + 1))
                gate = gate_t[:, P * t + n_s.start : P * t + n_s.stop]
                nc.vector.tensor_mul(
                    out=result[:, n_s].rearrange("p n (g x) -> p n g x", g=TRI),
                    in0=by_three[:, :, n_s].rearrange("p g n x -> p n g x"),
                    in1=gate.unsqueeze(2).unsqueeze(3).to_broadcast([P, P // parts, TRI, TRI]),
                )
                for i in range(BLKS):
                    o_lo = P * t + SQ * i
                    by_block = out_rows[SQ * blks * part : SQ * blks * (part + 1), PIX * o_lo : PIX * (o_lo + SQ)]
                    queue = nc.sync if i < BLKS // 2 else (nc.scalar if t == O_TILES - 1 else nc.gpsimd)
                    queue.dma_start(
                        out=by_block.rearrange("(j c) n -> c j n", c=SQ),
                        in_=result[SQ * i : SQ * (i + 1), n_s].rearrange("c (j r) x -> c j (r x)", j=blks),
                    )

        for t in range(O_TILES):
            normed = work.tile([P, COLS], F32, align_bytes=64)
            turned = work.tile([P, COLS], F32, align_bytes=64)
            by_three = work.tile([P, TRI, P, TRI], F32)
            copy = nc.scalar.copy if t < O_TILES - 1 else nc.vector.tensor_copy
            for k in all_banks:
                if t == 0:
                    acc = accs0[k]
                else:
                    acc = new_acc()
                    for g in range(PASSES):
                        multiply(t, acc, g, k)
                normalise(t, k, acc, normed)
                if t == O_TILES - 1 and k == 0:
                    gate_and_store(t - 1, before, 1)
                turn_squares(k, normed, turned)
                if 0 < t < O_TILES - 1 and k == len(all_banks) - 1:
                    gate_and_store(t - 1, before, 1)
                if k > 0:
                    interleave(copy, turned, by_three, k - 1)
            interleave(copy, turned, by_three, TRI - 1)
            before = by_three
            if t == 0:
                gate_finish(1)
        gate_and_store(O_TILES - 1, before, 2)
